import numpy as np
import ml_dtypes


def mxq(x, axis, fmt="e4m3"):
    dtype, down = {"e4m3": (ml_dtypes.float8_e4m3fn, 7), "e5m2": (ml_dtypes.float8_e5m2, 14)}[fmt]
    v = np.moveaxis(np.asarray(x, np.float32).astype(ml_dtypes.bfloat16).astype(np.float64), axis, -1)
    blocks = v.reshape(v.shape[:-1] + (-1, 32))
    amax = np.abs(blocks).max(-1, keepdims=True)
    byte = np.maximum(np.where(amax > 0, np.frexp(amax)[1] - 1 + 127, 0) - down, 1)
    scale = np.exp2(byte - 127.0)
    codes = (blocks / scale).astype(np.float32).astype(dtype).astype(np.float64)
    return np.moveaxis((codes * scale).reshape(v.shape), -1, axis)


WIDE = False


def mx_kscale(k):
    if not WIDE:
        return np.ones(k)
    levels = np.array([10, -10, 5, -5, 0])
    a = np.random.permutation(np.resize(levels, k // 512 * 4)).reshape(k // 512, 4)
    idx = np.arange(k)
    return np.exp2(a[idx // 512, idx % 128 // 32])


BF16 = ml_dtypes.bfloat16


def bf(x):
    return np.asarray(x, np.float32).astype(BF16)


def f64(x):
    return np.asarray(x).astype(np.float64)


E2M1 = np.array([0.0, 0.5, 1.0, 1.5, 2.0, 3.0, 4.0, 6.0, -0.0, -0.5, -1.0, -1.5, -2.0, -3.0, -4.0, -6.0])


def pack_weight(w, fmt):
    k, n = w.shape
    w = f64(bf(w)).reshape(k // 32, 32, n)
    amax = np.abs(w).max(1)
    if fmt == "e4m3":
        byte = np.frexp(amax)[1] - 1 + 127 - 7
    else:
        mant, ex = np.frexp(amax / 6.0)
        byte = np.where(mant > 0.5, ex, ex - 1) + 127
    byte = np.clip(np.where(amax > 0, byte, 1), 1, 254)
    scaled = (w * np.exp2(127.0 - byte)[:, None, :]).reshape(k, n).astype(np.float32)
    by_word = np.ascontiguousarray(scaled.reshape(k // 512, 128, 4, n).transpose(0, 1, 3, 2))
    if fmt == "e4m3":
        words = by_word.astype(ml_dtypes.float8_e4m3fn).view(np.uint8)
    else:
        c = by_word.astype(ml_dtypes.float4_e2m1fn).view(np.uint8) & 0xF
        words = c[..., 0::2] | (c[..., 1::2] << 4)
    return np.ascontiguousarray(words), np.ascontiguousarray(byte.astype(np.uint8).reshape(k // 512, 16, n))


def unpack_weight(words, scales, fmt):
    g, p, n, _ = words.shape
    if fmt == "e4m3":
        vals = np.ascontiguousarray(words).view(ml_dtypes.float8_e4m3fn).astype(np.float64)
    else:
        nib = np.empty((g, p, n, 4), np.uint8)
        nib[..., 0::2] = words & 0xF
        nib[..., 1::2] = words >> 4
        vals = E2M1[nib]
    vals = vals * np.repeat(np.exp2(scales.astype(np.float64) - 127.0), 8, axis=1)[..., None]
    return vals.transpose(0, 1, 3, 2).reshape(g * 512, n)

def pack4(w):
    words, scales = pack_weight(w, "e2m1")
    return words.reshape(words.shape[0], 128, -1), scales


def unpack4(words, scales):
    return unpack_weight(words.reshape(words.shape[0], 128, -1, 2), scales, "e2m1")


B, S, H, NH, FF = 8, 512, 1024, 8, 1024
EPS = 1e-7


def layer_norm(x, g, b):
    m = x.mean(-1, keepdims=True)
    v = ((x - m) ** 2).mean(-1, keepdims=True)
    return (x - m) / np.sqrt(v + EPS) * g + b


def setup_inputs():
    s = mx_kscale(FF)
    r = np.random.standard_normal
    ff = bf(r((B, S, FF)) * 0.65 * s)
    attn_out = bf(r((B, S, H)))
    Wf_words, Wf_scales = pack4(r((FF, H)) * 1.5 / np.sqrt(FF) / s[:, None])
    return {"ff": ff, "attn_out": attn_out,
            "Wf_words": Wf_words, "Wf_scales": Wf_scales, "b_f": bf(r(H) * 0.2),
            "ln2_g": bf(1.0 + 0.1 * r(H)), "ln2_b": bf(0.1 * r(H))}


def reference(ff, attn_out, Wf_words, Wf_scales, b_f, ln2_g, ln2_b):
    u = (mxq(f64(ff), 2, "e4m3") @ unpack4(Wf_words, Wf_scales)) + f64(b_f) + f64(attn_out)
    return layer_norm(u, f64(ln2_g), f64(ln2_b))

@@ -1,0 +1,275 @@
+from contextlib import ExitStack
+
+import concourse.mybir as mybir
+from concourse.masks import make_identity
+
+F32 = mybir.dt.float32
+BF16 = mybir.dt.bfloat16
+I32 = mybir.dt.int32
+U32 = mybir.dt.uint32
+U8 = mybir.dt.uint8
+FP8X4 = mybir.dt.float8_e4m3fn_x4
+FP4X4 = mybir.dt.float4_e2m1fn_x4
+ADD = mybir.AluOpType.add
+MULT = mybir.AluOpType.mult
+ACT = mybir.ActivationFunctionType
+
+P = 128
+TOKENS = 8 * 512
+K = 1024
+H = 1024
+EPS = 1e-7
+PACK = 4
+K_PASS = P * PACK
+PASSES = K // K_PASS
+BANK = 512
+HALVES = H // BANK
+TILES_PER_CHUNK = 4
+CHUNKS = TOKENS // (P * TILES_PER_CHUNK)
+TILES = CHUNKS * TILES_PER_CHUNK
+
+FLOPS = 2 * TOKENS * K * H
+
+FF_LOAD_LEAD = 14
+ATTN_LOAD_LEAD = 10
+TRANSPOSE_LEAD = 6
+REGROUP_LEAD = 5
+QUANTISE_LEAD = 2
+BIAS_LEAD = 2
+MULTIPLY_LEAD = 1
+SHIFT_LAG = 1
+
+
+def tile_disentangledattention_pc_t_kernel(
+    tc, ff, attn_out, Wf_words, Wf_scales, b_f, ln2_g, ln2_b, out
+):
+    nc = tc.nc
+    ff_chunks = ff.flatten_outer_dims().rearrange(
+        "(c p j) k -> c p j k", p=P, j=TILES_PER_CHUNK
+    )
+    attn_chunks = attn_out.flatten_outer_dims().rearrange(
+        "(c p j) n -> c p j n", p=P, j=TILES_PER_CHUNK
+    )
+    out_tiles = out.flatten_outer_dims().rearrange(
+        "(c p j) n -> c j p n", p=P, j=TILES_PER_CHUNK
+    )
+
+    with ExitStack() as ctx:
+        ctx.enter_context(tc.manual_schedule())
+        consts = ctx.enter_context(tc.tile_pool(name="consts", bufs=1))
+        loads = ctx.enter_context(tc.tile_pool(name="loads", bufs=3))
+        quant = ctx.enter_context(tc.tile_pool(name="quant", bufs=2))
+        work = ctx.enter_context(tc.tile_pool(name="work", bufs=3))
+        stats = ctx.enter_context(tc.tile_pool(name="stats", bufs=4))
+        psum_const = ctx.enter_context(tc.psum_pool(name="psum_const", bufs=1))
+        psum_acc = ctx.enter_context(tc.psum_pool(name="psum_acc", bufs=2 * HALVES))
+        psum_xt = ctx.enter_context(tc.psum_pool(name="psum_xt", bufs=2))
+
+        ff_of = {}
+        attn_of = {}
+        xt_of = {}
+        grouped_of = {}
+        codes_of = {}
+        planes_of = {}
+        acc_of = {}
+        r_of = {}
+        u_of = {}
+        w_of = {}
+        negmean_of = {}
+        std_of = {}
+
+        def load_ff(c):
+            ff_sb = loads.tile([P, TILES_PER_CHUNK, K], BF16)
+            nc.sync.dma_start(out=ff_sb[:], in_=ff_chunks[c])
+            ff_of[c] = ff_sb
+
+        def load_attn(c):
+            attn_sb = loads.tile([P, TILES_PER_CHUNK, H], BF16)
+            nc.sync.dma_start(out=attn_sb[:], in_=attn_chunks[c])
+            attn_of[c] = attn_sb
+
+        load_ff(0)
+
+        w_words = consts.tile([P, PASSES, 2 * H], U8, align_bytes=64)
+        nc.sync.dma_start(
+            out=w_words[:].bitcast(I32),
+            in_=Wf_words.rearrange("g p b -> p g b").bitcast(I32),
+        )
+        w_planes = consts.tile([P, PASSES, H], U8, align_bytes=64)
+        nc.vector.memset(w_planes[:].bitcast(I32), 0)
+        for quadrant in range(4):
+            nc.sync.dma_start(
+                out=w_planes[32 * quadrant : 32 * quadrant + 4].bitcast(I32),
+                in_=Wf_scales[:, 4 * quadrant : 4 * quadrant + 4, :]
+                .rearrange("g r n -> r g n")
+                .bitcast(I32),
+            )
+
+        rows = consts.tile([P, 3, H], BF16)
+        nc.vector.memset(rows[:].bitcast(I32), 0)
+        for v, vector in enumerate((ln2_g, ln2_b, b_f)):
+            nc.sync.dma_start(out=rows[0:1, v, :], in_=vector.unsqueeze(0))
+        ones = consts.tile([P, P], BF16)
+        nc.vector.memset(ones[:], 1.0)
+        eps = consts.tile([P, 1], F32)
+        nc.vector.memset(eps[:], EPS)
+        ident = consts.tile([P, P], F32)
+        make_identity(nc, ident[:])
+
+        gain_ps = psum_const.tile([P, H], BF16)
+        shift_ps = psum_const.tile([P, H], BF16)
+        bias_sb = consts.tile([P, H], BF16)
+        for h in range(HALVES):
+            cols = slice(h * BANK, (h + 1) * BANK)
+            nc.tensor.matmul(out=gain_ps[:, cols], lhsT=ones[:], rhs=rows[:, 0, cols], start=True, stop=True)
+            nc.tensor.matmul(out=shift_ps[:, cols], lhsT=ones[:], rhs=rows[:, 1, cols], start=True, stop=True)
+            acc = psum_acc.tile([P, BANK], F32)
+            nc.tensor.matmul(out=acc[:], lhsT=ones[:], rhs=rows[:, 2, cols], start=True, stop=True)
+            nc.scalar.copy(out=bias_sb[:, cols], in_=acc[:])
+
+        def transpose(t):
+            c, j = divmod(t, TILES_PER_CHUNK)
+            words = ff_of[c][:, j, :].bitcast(F32)
+            xt = psum_xt.tile([P, 2 * PASSES, P], F32)
+            for g in range(PASSES):
+                for u in range(2):
+                    nc.tensor.transpose(
+                        xt[:, 2 * g + u, :],
+                        words[:, 256 * g + u : 256 * (g + 1) : 2],
+                        ident[:],
+                    )
+            xt_of[t] = xt
+
+        def regroup(t):
+            c, j = divmod(t, TILES_PER_CHUNK)
+            if j == 0:
+                grouped = quant.tile([P, TILES_PER_CHUNK, PASSES, P, PACK], BF16, align_bytes=64)
+                grouped_of[c] = grouped
+            nc.scalar.copy(
+                out=grouped_of[c][:, j].bitcast(F32),
+                in_=xt_of[t][:].rearrange("p (g u) r -> p g r u", u=2),
+            )
+
+        def quantise(c):
+            codes = quant.tile([P, TILES_PER_CHUNK, PASSES, P], U32, align_bytes=64)
+            planes = quant.tile([P, TILES_PER_CHUNK, PASSES, P], U8, align_bytes=64)
+            nc.vector.quantize_mx(
+                out=codes[:].rearrange("p j g r -> p (j g r)").bitcast(FP8X4),
+                scales=planes[:].rearrange("p j g r -> p (j g r)"),
+                in_=grouped_of[c][:].rearrange("p j g r t -> p (j g r t)"),
+            )
+            codes_of[c] = codes
+            planes_of[c] = planes
+
+        def multiply(t):
+            c, j = divmod(t, TILES_PER_CHUNK)
+            for h in range(HALVES):
+                acc = psum_acc.tile([P, BANK], F32)
+                for g in range(PASSES):
+                    nc.tensor.matmul_mx(
+                        out=acc[:],
+                        lhsT=codes_of[c][:, j, g, :].bitcast(FP8X4),
+                        lhsT_scale=planes_of[c][:, j, g, :],
+                        rhs=w_words[:, g, 2 * h * BANK : 2 * (h + 1) * BANK].bitcast(FP4X4),
+                        rhs_scale=w_planes[:, g, h * BANK : (h + 1) * BANK],
+                        start=(g == 0),
+                        stop=(g == PASSES - 1),
+                    )
+                acc_of[(t, h)] = acc
+
+        def add_bias(t):
+            c, j = divmod(t, TILES_PER_CHUNK)
+            r = work.tile([P, H], F32)
+            nc.gpsimd.tensor_tensor(out=r[:], in0=attn_of[c][:, j, :], in1=bias_sb[:], op=ADD)
+            r_of[t] = r
+
+        def add_residual(t):
+            u = work.tile([P, H], F32)
+            sums = stats.tile([P, HALVES], F32)
+            for h in range(HALVES):
+                cols = slice(h * BANK, (h + 1) * BANK)
+                nc.vector.scalar_tensor_tensor(
+                    out=u[:, cols],
+                    in0=acc_of[(t, h)][:],
+                    scalar=0.0,
+                    in1=r_of[t][:, cols],
+                    op0=ADD,
+                    op1=ADD,
+                    accum_out=sums[:, h : h + 1],
+                )
+            u_of[t] = u
+            return sums
+
+        def statistics(t, sums):
+            scaled = stats.tile([P, HALVES], F32)
+            negmean = stats.tile([P, 1], F32)
+            nc.scalar.activation(
+                out=scaled[:], in_=sums[:], func=ACT.Identity, scale=-1.0 / H, accum_out=negmean[:]
+            )
+            squares = work.tile([P, H], BF16)
+            ssq = stats.tile([P, 1], F32)
+            nc.scalar.activation(
+                out=squares[:], in_=u_of[t][:], func=ACT.Square, bias=negmean[:], accum_out=ssq[:]
+            )
+            std = stats.tile([P, 1], F32)
+            nc.scalar.activation(out=std[:], in_=ssq[:], func=ACT.Sqrt, bias=eps[:], scale=1.0 / H)
+            negmean_of[t] = negmean
+            std_of[t] = std
+
+        def centre_and_gain(t):
+            w = work.tile([P, H], F32)
+            nc.vector.scalar_tensor_tensor(
+                out=w[:], in0=u_of[t][:], scalar=negmean_of[t][:], in1=gain_ps[:], op0=ADD, op1=MULT
+            )
+            w_of[t] = w
+
+        def scale_shift_store(t):
+            c, j = divmod(t, TILES_PER_CHUNK)
+            rstd = stats.tile([P, 1], F32)
+            nc.vector.reciprocal(out=rstd[:], in_=std_of[t][:])
+            y = work.tile([P, H], F32)
+            nc.vector.scalar_tensor_tensor(
+                out=y[:], in0=w_of[t][:], scalar=rstd[:], in1=shift_ps[:], op0=MULT, op1=ADD
+            )
+            nc.sync.dma_start(out=out_tiles[c, j], in_=y[:])
+
+        def chunk_due(step, lead):
+            c, j = divmod(step + lead, TILES_PER_CHUNK)
+            return c if j == 0 and 0 <= c < CHUNKS else None
+
+        def tile_due(step, lead):
+            t = step + lead
+            return t if 0 <= t < TILES else None
+
+        for step in range(-ATTN_LOAD_LEAD, TILES + SHIFT_LAG):
+            c = chunk_due(step, FF_LOAD_LEAD)
+            if c is not None:
+                load_ff(c)
+            c = chunk_due(step, ATTN_LOAD_LEAD)
+            if c is not None:
+                load_attn(c)
+            t = tile_due(step, TRANSPOSE_LEAD)
+            if t is not None:
+                transpose(t)
+            t = tile_due(step, REGROUP_LEAD)
+            if t is not None:
+                regroup(t)
+            t = tile_due(step, BIAS_LEAD)
+            if t is not None:
+                add_bias(t)
+            now = tile_due(step, 0)
+            if now is not None:
+                sums = add_residual(now)
+            c = chunk_due(step, QUANTISE_LEAD)
+            if c is not None:
+                quantise(c)
+            t = tile_due(step, MULTIPLY_LEAD)
+            if t is not None:
+                multiply(t)
+            if now is not None:
+                statistics(now, sums)
+            t = tile_due(step, -SHIFT_LAG)
+            if t is not None:
+                scale_shift_store(t)
+            if now is not None:
+                centre_and_gain(now)

@@ -24,14 +24,13 @@ K_PASS = P * PACK
 PASSES = K // K_PASS
 BANK = 512
 HALVES = H // BANK
-TILES_PER_CHUNK = 4
-CHUNKS = TOKENS // (P * TILES_PER_CHUNK)
-TILES = CHUNKS * TILES_PER_CHUNK
+TILES = TOKENS // P
+GROUP = 4
+GROUPS = TILES // GROUP
+AHEAD = 4
 
 FLOPS = 2 * TOKENS * K * H
 
-FF_LOAD_LEAD = 14
-ATTN_LOAD_LEAD = 10
 TRANSPOSE_LEAD = 6
 REGROUP_LEAD = 5
 QUANTISE_LEAD = 2
@@ -44,20 +43,14 @@ def tile_disentangledattention_pc_t_kernel(
     tc, ff, attn_out, Wf_words, Wf_scales, b_f, ln2_g, ln2_b, out
 ):
     nc = tc.nc
-    ff_chunks = ff.flatten_outer_dims().rearrange(
-        "(c p j) k -> c p j k", p=P, j=TILES_PER_CHUNK
-    )
-    attn_chunks = attn_out.flatten_outer_dims().rearrange(
-        "(c p j) n -> c p j n", p=P, j=TILES_PER_CHUNK
-    )
-    out_tiles = out.flatten_outer_dims().rearrange(
-        "(c p j) n -> c j p n", p=P, j=TILES_PER_CHUNK
-    )
+    ff_tiles = ff.flatten_outer_dims().rearrange("(t p) k -> t p k", p=P)
+    attn_tiles = attn_out.flatten_outer_dims().rearrange("(t p) n -> t p n", p=P)
+    out_tiles = out.flatten_outer_dims().rearrange("(t p) n -> t p n", p=P)
 
     with ExitStack() as ctx:
         ctx.enter_context(tc.manual_schedule())
         consts = ctx.enter_context(tc.tile_pool(name="consts", bufs=1))
-        loads = ctx.enter_context(tc.tile_pool(name="loads", bufs=3))
+        loads = ctx.enter_context(tc.tile_pool(name="loads", bufs=AHEAD + 1))
         quant = ctx.enter_context(tc.tile_pool(name="quant", bufs=2))
         work = ctx.enter_context(tc.tile_pool(name="work", bufs=3))
         stats = ctx.enter_context(tc.tile_pool(name="stats", bufs=4))
@@ -76,19 +69,27 @@ def tile_disentangledattention_pc_t_kernel(
         u_of = {}
         w_of = {}
         negmean_of = {}
-        std_of = {}
+        rstd_of = {}
 
-        def load_ff(c):
-            ff_sb = loads.tile([P, TILES_PER_CHUNK, K], BF16)
-            nc.sync.dma_start(out=ff_sb[:], in_=ff_chunks[c])
-            ff_of[c] = ff_sb
+        def load_ff(t):
+            if t < TILES:
+                ff_sb = loads.tile([P, K], BF16)
+                nc.sync.dma_start(out=ff_sb[:], in_=ff_tiles[t])
+                ff_of[t] = ff_sb
 
-        def load_attn(c):
-            attn_sb = loads.tile([P, TILES_PER_CHUNK, H], BF16)
-            nc.sync.dma_start(out=attn_sb[:], in_=attn_chunks[c])
-            attn_of[c] = attn_sb
+        def load_attn(t):
+            if t < TILES:
+                attn_sb = loads.tile([P, H], BF16)
+                nc.sync.dma_start(out=attn_sb[:], in_=attn_tiles[t])
+                attn_of[t] = attn_sb
 
-        load_ff(0)
+        for t in range(AHEAD):
+            load_ff(t)
+
+        rows = consts.tile([P, 3, H], BF16)
+        nc.vector.memset(rows[:].bitcast(I32), 0)
+        for v, vector in enumerate((ln2_g, ln2_b, b_f)):
+            nc.sync.dma_start(out=rows[0:1, v, :], in_=vector.unsqueeze(0))
 
         w_words = consts.tile([P, PASSES, 2 * H], U8, align_bytes=64)
         nc.sync.dma_start(
@@ -105,10 +106,9 @@ def tile_disentangledattention_pc_t_kernel(
                 .bitcast(I32),
             )
 
-        rows = consts.tile([P, 3, H], BF16)
-        nc.vector.memset(rows[:].bitcast(I32), 0)
-        for v, vector in enumerate((ln2_g, ln2_b, b_f)):
-            nc.sync.dma_start(out=rows[0:1, v, :], in_=vector.unsqueeze(0))
+        for t in range(AHEAD):
+            load_attn(t)
+
         ones = consts.tile([P, P], BF16)
         nc.vector.memset(ones[:], 1.0)
         eps = consts.tile([P, 1], F32)
@@ -128,8 +128,7 @@ def tile_disentangledattention_pc_t_kernel(
             nc.scalar.copy(out=bias_sb[:, cols], in_=acc[:])
 
         def transpose(t):
-            c, j = divmod(t, TILES_PER_CHUNK)
-            words = ff_of[c][:, j, :].bitcast(F32)
+            words = ff_of[t][:].bitcast(F32)
             xt = psum_xt.tile([P, 2 * PASSES, P], F32)
             for g in range(PASSES):
                 for u in range(2):
@@ -139,11 +138,12 @@ def tile_disentangledattention_pc_t_kernel(
                         ident[:],
                     )
             xt_of[t] = xt
+            load_ff(t + AHEAD)
 
         def regroup(t):
-            c, j = divmod(t, TILES_PER_CHUNK)
+            c, j = divmod(t, GROUP)
             if j == 0:
-                grouped = quant.tile([P, TILES_PER_CHUNK, PASSES, P, PACK], BF16, align_bytes=64)
+                grouped = quant.tile([P, GROUP, PASSES, P, PACK], BF16, align_bytes=64)
                 grouped_of[c] = grouped
             nc.scalar.copy(
                 out=grouped_of[c][:, j].bitcast(F32),
@@ -151,8 +151,8 @@ def tile_disentangledattention_pc_t_kernel(
             )
 
         def quantise(c):
-            codes = quant.tile([P, TILES_PER_CHUNK, PASSES, P], U32, align_bytes=64)
-            planes = quant.tile([P, TILES_PER_CHUNK, PASSES, P], U8, align_bytes=64)
+            codes = quant.tile([P, GROUP, PASSES, P], U32, align_bytes=64)
+            planes = quant.tile([P, GROUP, PASSES, P], U8, align_bytes=64)
             nc.vector.quantize_mx(
                 out=codes[:].rearrange("p j g r -> p (j g r)").bitcast(FP8X4),
                 scales=planes[:].rearrange("p j g r -> p (j g r)"),
@@ -162,7 +162,7 @@ def tile_disentangledattention_pc_t_kernel(
             planes_of[c] = planes
 
         def multiply(t):
-            c, j = divmod(t, TILES_PER_CHUNK)
+            c, j = divmod(t, GROUP)
             for h in range(HALVES):
                 acc = psum_acc.tile([P, BANK], F32)
                 for g in range(PASSES):
@@ -178,10 +178,10 @@ def tile_disentangledattention_pc_t_kernel(
                 acc_of[(t, h)] = acc
 
         def add_bias(t):
-            c, j = divmod(t, TILES_PER_CHUNK)
             r = work.tile([P, H], F32)
-            nc.gpsimd.tensor_tensor(out=r[:], in0=attn_of[c][:, j, :], in1=bias_sb[:], op=ADD)
+            nc.gpsimd.tensor_tensor(out=r[:], in0=attn_of[t][:], in1=bias_sb[:], op=ADD)
             r_of[t] = r
+            load_attn(t + AHEAD)
 
         def add_residual(t):
             u = work.tile([P, H], F32)
@@ -211,10 +211,12 @@ def tile_disentangledattention_pc_t_kernel(
             nc.scalar.activation(
                 out=squares[:], in_=u_of[t][:], func=ACT.Square, bias=negmean[:], accum_out=ssq[:]
             )
-            std = stats.tile([P, 1], F32)
-            nc.scalar.activation(out=std[:], in_=ssq[:], func=ACT.Sqrt, bias=eps[:], scale=1.0 / H)
+            rstd = stats.tile([P, 1], F32)
+            nc.scalar.activation(
+                out=rstd[:], in_=ssq[:], func=ACT.Abs_reciprocal_sqrt, bias=eps[:], scale=1.0 / H
+            )
             negmean_of[t] = negmean
-            std_of[t] = std
+            rstd_of[t] = rstd
 
         def centre_and_gain(t):
             w = work.tile([P, H], F32)
@@ -224,30 +226,21 @@ def tile_disentangledattention_pc_t_kernel(
             w_of[t] = w
 
         def scale_shift_store(t):
-            c, j = divmod(t, TILES_PER_CHUNK)
-            rstd = stats.tile([P, 1], F32)
-            nc.vector.reciprocal(out=rstd[:], in_=std_of[t][:])
             y = work.tile([P, H], F32)
             nc.vector.scalar_tensor_tensor(
-                out=y[:], in0=w_of[t][:], scalar=rstd[:], in1=shift_ps[:], op0=MULT, op1=ADD
+                out=y[:], in0=w_of[t][:], scalar=rstd_of[t][:], in1=shift_ps[:], op0=MULT, op1=ADD
             )
-            nc.sync.dma_start(out=out_tiles[c, j], in_=y[:])
+            nc.sync.dma_start(out=out_tiles[t], in_=y[:])
 
-        def chunk_due(step, lead):
-            c, j = divmod(step + lead, TILES_PER_CHUNK)
-            return c if j == 0 and 0 <= c < CHUNKS else None
+        def group_due(step, lead):
+            c, j = divmod(step + lead, GROUP)
+            return c if j == 0 and 0 <= c < GROUPS else None
 
         def tile_due(step, lead):
             t = step + lead
             return t if 0 <= t < TILES else None
 
-        for step in range(-ATTN_LOAD_LEAD, TILES + SHIFT_LAG):
-            c = chunk_due(step, FF_LOAD_LEAD)
-            if c is not None:
-                load_ff(c)
-            c = chunk_due(step, ATTN_LOAD_LEAD)
-            if c is not None:
-                load_attn(c)
+        for step in range(-TRANSPOSE_LEAD, TILES + SHIFT_LAG):
             t = tile_due(step, TRANSPOSE_LEAD)
             if t is not None:
                 transpose(t)
@@ -260,7 +253,7 @@ def tile_disentangledattention_pc_t_kernel(
             now = tile_due(step, 0)
             if now is not None:
                 sums = add_residual(now)
-            c = chunk_due(step, QUANTISE_LEAD)
+            c = group_due(step, QUANTISE_LEAD)
             if c is not None:
                 quantise(c)
             t = tile_due(step, MULTIPLY_LEAD)

@@ -28,13 +28,15 @@ TILES = TOKENS // P
 GROUP = 4
 GROUPS = TILES // GROUP
 AHEAD = 4
+ATTN_LEAD = 7
+ATTN_BUFS = 8
+R_BUFS = 6
 
 FLOPS = 2 * TOKENS * K * H
 
 TRANSPOSE_LEAD = 6
 REGROUP_LEAD = 5
 QUANTISE_LEAD = 2
-BIAS_LEAD = 2
 MULTIPLY_LEAD = 1
 SHIFT_LAG = 1
 
@@ -51,6 +53,8 @@ def tile_disentangledattention_pc_t_kernel(
         ctx.enter_context(tc.manual_schedule())
         consts = ctx.enter_context(tc.tile_pool(name="consts", bufs=1))
         loads = ctx.enter_context(tc.tile_pool(name="loads", bufs=AHEAD + 1))
+        attn_loads = ctx.enter_context(tc.tile_pool(name="attn_loads", bufs=ATTN_BUFS))
+        resid = ctx.enter_context(tc.tile_pool(name="resid", bufs=R_BUFS))
         quant = ctx.enter_context(tc.tile_pool(name="quant", bufs=2))
         work = ctx.enter_context(tc.tile_pool(name="work", bufs=3))
         stats = ctx.enter_context(tc.tile_pool(name="stats", bufs=4))
@@ -79,7 +83,7 @@ def tile_disentangledattention_pc_t_kernel(
 
         def load_attn(t):
             if t < TILES:
-                attn_sb = loads.tile([P, H], BF16)
+                attn_sb = attn_loads.tile([P, H], BF16)
                 nc.sync.dma_start(out=attn_sb[:], in_=attn_tiles[t])
                 attn_of[t] = attn_sb
 
@@ -106,7 +110,7 @@ def tile_disentangledattention_pc_t_kernel(
                 .bitcast(I32),
             )
 
-        for t in range(AHEAD):
+        for t in range(ATTN_LEAD - TRANSPOSE_LEAD):
             load_attn(t)
 
         ones = consts.tile([P, P], BF16)
@@ -160,6 +164,10 @@ def tile_disentangledattention_pc_t_kernel(
             )
             codes_of[c] = codes
             planes_of[c] = planes
+            gate = stats.tile([P, 1], U32)
+            nc.gpsimd.tensor_copy(out=gate[:], in_=codes[:, 0, 0, 0:1])
+            for j in range(GROUP):
+                add_bias(GROUP * c + j)
 
         def multiply(t):
             c, j = divmod(t, GROUP)
@@ -178,10 +186,9 @@ def tile_disentangledattention_pc_t_kernel(
                 acc_of[(t, h)] = acc
 
         def add_bias(t):
-            r = work.tile([P, H], F32)
+            r = resid.tile([P, H], F32)
             nc.gpsimd.tensor_tensor(out=r[:], in0=attn_of[t][:], in1=bias_sb[:], op=ADD)
             r_of[t] = r
-            load_attn(t + AHEAD)
 
         def add_residual(t):
             u = work.tile([P, H], F32)
@@ -247,9 +254,7 @@ def tile_disentangledattention_pc_t_kernel(
             t = tile_due(step, REGROUP_LEAD)
             if t is not None:
                 regroup(t)
-            t = tile_due(step, BIAS_LEAD)
-            if t is not None:
-                add_bias(t)
+            load_attn(step + ATTN_LEAD)
             now = tile_due(step, 0)
             if now is not None:
                 sums = add_residual(now)

@@ -30,7 +30,8 @@ GROUPS = TILES // GROUP
 AHEAD = 4
 ATTN_LEAD = 7
 ATTN_BUFS = 8
-R_BUFS = 6
+R_BUFS = 7
+STORE_LAG = 3
 
 FLOPS = 2 * TOKENS * K * H
 
@@ -55,6 +56,7 @@ def tile_disentangledattention_pc_t_kernel(
         loads = ctx.enter_context(tc.tile_pool(name="loads", bufs=AHEAD + 1))
         attn_loads = ctx.enter_context(tc.tile_pool(name="attn_loads", bufs=ATTN_BUFS))
         resid = ctx.enter_context(tc.tile_pool(name="resid", bufs=R_BUFS))
+        offload = ctx.enter_context(tc.tile_pool(name="offload", bufs=2))
         quant = ctx.enter_context(tc.tile_pool(name="quant", bufs=2))
         work = ctx.enter_context(tc.tile_pool(name="work", bufs=3))
         stats = ctx.enter_context(tc.tile_pool(name="stats", bufs=4))
@@ -74,6 +76,7 @@ def tile_disentangledattention_pc_t_kernel(
         w_of = {}
         negmean_of = {}
         rstd_of = {}
+        y_late_of = {}
 
         def load_ff(t):
             if t < TILES:
@@ -130,6 +133,8 @@ def tile_disentangledattention_pc_t_kernel(
             acc = psum_acc.tile([P, BANK], F32)
             nc.tensor.matmul(out=acc[:], lhsT=ones[:], rhs=rows[:, 2, cols], start=True, stop=True)
             nc.scalar.copy(out=bias_sb[:, cols], in_=acc[:])
+        shift_sb = consts.tile([P, H], BF16)
+        nc.scalar.copy(out=shift_sb[:], in_=shift_ps[:])
 
         def transpose(t):
             words = ff_of[t][:].bitcast(F32)
@@ -166,8 +171,6 @@ def tile_disentangledattention_pc_t_kernel(
             planes_of[c] = planes
             gate = stats.tile([P, 1], U32)
             nc.gpsimd.tensor_copy(out=gate[:], in_=codes[:, 0, 0, 0:1])
-            for j in range(GROUP):
-                add_bias(GROUP * c + j)
 
         def multiply(t):
             c, j = divmod(t, GROUP)
@@ -186,6 +189,8 @@ def tile_disentangledattention_pc_t_kernel(
                 acc_of[(t, h)] = acc
 
         def add_bias(t):
+            if t >= TILES:
+                return
             r = resid.tile([P, H], F32)
             nc.gpsimd.tensor_tensor(out=r[:], in0=attn_of[t][:], in1=bias_sb[:], op=ADD)
             r_of[t] = r
@@ -239,6 +244,16 @@ def tile_disentangledattention_pc_t_kernel(
             )
             nc.sync.dma_start(out=out_tiles[t], in_=y[:])
 
+        def shared_out(t):
+            return (t + SHIFT_LAG + QUANTISE_LEAD) % GROUP == 0
+
+        def scale_on_scalar_shift_on_gpsimd(t):
+            scaled_w = offload.tile([P, H], F32)
+            nc.scalar.activation(out=scaled_w[:], in_=w_of[t][:], func=ACT.Identity, scale=rstd_of[t][:])
+            y_late = offload.tile([P, H], F32)
+            nc.gpsimd.tensor_tensor(out=y_late[:], in0=scaled_w[:], in1=shift_sb[:], op=ADD)
+            y_late_of[t] = y_late
+
         def group_due(step, lead):
             c, j = divmod(step + lead, GROUP)
             return c if j == 0 and 0 <= c < GROUPS else None
@@ -247,7 +262,8 @@ def tile_disentangledattention_pc_t_kernel(
             t = step + lead
             return t if 0 <= t < TILES else None
 
-        for step in range(-TRANSPOSE_LEAD, TILES + SHIFT_LAG):
+        add_bias(0)
+        for step in range(-TRANSPOSE_LEAD, TILES + STORE_LAG):
             t = tile_due(step, TRANSPOSE_LEAD)
             if t is not None:
                 transpose(t)
@@ -266,8 +282,19 @@ def tile_disentangledattention_pc_t_kernel(
                 multiply(t)
             if now is not None:
                 statistics(now, sums)
+            if c is not None:
+                add_bias(GROUP * c + 1)
             t = tile_due(step, -SHIFT_LAG)
             if t is not None:
-                scale_shift_store(t)
+                if shared_out(t):
+                    scale_on_scalar_shift_on_gpsimd(t)
+                else:
+                    scale_shift_store(t)
+            if c is not None:
+                for j in range(2, GROUP + 1):
+                    add_bias(GROUP * c + j)
             if now is not None:
                 centre_and_gain(now)
+            t = tile_due(step, -STORE_LAG)
+            if t is not None and shared_out(t):
+                nc.sync.dma_start(out=out_tiles[t], in_=y_late_of[t][:])

@@ -25,21 +25,35 @@ PASSES = K // K_PASS
 BANK = 512
 HALVES = H // BANK
 TILES = TOKENS // P
-GROUP = 4
-GROUPS = TILES // GROUP
-AHEAD = 4
-ATTN_LEAD = 7
-ATTN_BUFS = 8
-R_BUFS = 7
-STORE_LAG = 3
+
+GROUP_SIZES = (1, 1, 2, 2, 2) + (4,) * 6
+RG_SLACK = 1
+TS_MOD = 3; TS_PHASE = 0; TS_FROM = 6
+TS_LEAD0 = 3; TS_LEAD1 = 2
+ORDER = 0
+SPREAD_AT = 0; COPY_AT = 2
+ACC_BUFS = 3; XT_BUFS = 2; RP_BUFS = 1
+EVAC_LATE = 0
+PROD_LATE = 0
+TS_SPLIT = 0
+P0_MODE = 0
+P0_LEAD = 3
+assert sum(GROUP_SIZES) == TILES
 
 FLOPS = 2 * TOKENS * K * H
 
-TRANSPOSE_LEAD = 6
-REGROUP_LEAD = 5
+FF_LEAD = 9
+ATTN_LEAD = 7
 QUANTISE_LEAD = 2
 MULTIPLY_LEAD = 1
-SHIFT_LAG = 1
+TENSOR_SUM_LEAD = 3
+GAIN_LAG = 1
+SHIFT_LAG = 2
+LATE_SUM_LAG = 3
+STORE_LAG = 4
+FF_BUFS = 7
+ATTN_BUFS = 8
+R_BUFS = 7
 
 
 def tile_disentangledattention_pc_t_kernel(
@@ -50,19 +64,37 @@ def tile_disentangledattention_pc_t_kernel(
     attn_tiles = attn_out.flatten_outer_dims().rearrange("(t p) n -> t p n", p=P)
     out_tiles = out.flatten_outer_dims().rearrange("(t p) n -> t p n", p=P)
 
+    place_of = {}
+    last_of = {}
+    quantise_at = {}
+    regroup_at = {}
+    transpose_at = {}
+    first = 0
+    for c, size in enumerate(GROUP_SIZES):
+        quantise_at[first - QUANTISE_LEAD] = c
+        last_of[c] = first + size - 1
+        for j in range(size):
+            place_of[first + j] = (c, j)
+            due = first - QUANTISE_LEAD - (size - 1 - j) - (RG_SLACK if size > 2 else 0)
+            regroup_at.setdefault(due, []).append(first + j)
+            transpose_at.setdefault(due - 1, []).append(first + j)
+        first += size
+    first_step = min(transpose_at)
+
     with ExitStack() as ctx:
         ctx.enter_context(tc.manual_schedule())
         consts = ctx.enter_context(tc.tile_pool(name="consts", bufs=1))
-        loads = ctx.enter_context(tc.tile_pool(name="loads", bufs=AHEAD + 1))
+        ff_loads = ctx.enter_context(tc.tile_pool(name="ff_loads", bufs=FF_BUFS))
         attn_loads = ctx.enter_context(tc.tile_pool(name="attn_loads", bufs=ATTN_BUFS))
         resid = ctx.enter_context(tc.tile_pool(name="resid", bufs=R_BUFS))
-        offload = ctx.enter_context(tc.tile_pool(name="offload", bufs=2))
+        offload = ctx.enter_context(tc.tile_pool(name="offload", bufs=3))
         quant = ctx.enter_context(tc.tile_pool(name="quant", bufs=2))
-        work = ctx.enter_context(tc.tile_pool(name="work", bufs=3))
-        stats = ctx.enter_context(tc.tile_pool(name="stats", bufs=4))
+        work = ctx.enter_context(tc.tile_pool(name="work", bufs=4))
+        stats = ctx.enter_context(tc.tile_pool(name="stats", bufs=6))
         psum_const = ctx.enter_context(tc.psum_pool(name="psum_const", bufs=1))
-        psum_acc = ctx.enter_context(tc.psum_pool(name="psum_acc", bufs=2 * HALVES))
-        psum_xt = ctx.enter_context(tc.psum_pool(name="psum_xt", bufs=2))
+        psum_acc = ctx.enter_context(tc.psum_pool(name="psum_acc", bufs=ACC_BUFS))
+        psum_r = ctx.enter_context(tc.psum_pool(name="psum_r", bufs=RP_BUFS))
+        psum_xt = ctx.enter_context(tc.psum_pool(name="psum_xt", bufs=XT_BUFS))
 
         ff_of = {}
         attn_of = {}
@@ -77,10 +109,11 @@ def tile_disentangledattention_pc_t_kernel(
         negmean_of = {}
         rstd_of = {}
         y_late_of = {}
+        scaled_w_of = {}
 
         def load_ff(t):
             if t < TILES:
-                ff_sb = loads.tile([P, K], BF16)
+                ff_sb = ff_loads.tile([P, K], BF16)
                 nc.sync.dma_start(out=ff_sb[:], in_=ff_tiles[t])
                 ff_of[t] = ff_sb
 
@@ -90,21 +123,25 @@ def tile_disentangledattention_pc_t_kernel(
                 nc.sync.dma_start(out=attn_sb[:], in_=attn_tiles[t])
                 attn_of[t] = attn_sb
 
-        for t in range(AHEAD):
-            load_ff(t)
+        ones = consts.tile([P, P], BF16)
+        nc.vector.memset(ones[:], 1.0)
+        row_of = {}
+        for name, vector in (("bias", b_f), ("gain", ln2_g), ("shift", ln2_b)):
+            row = consts.tile([P, H], BF16, name="row_" + name)
+            nc.vector.memset(row[:].bitcast(I32), 0)
+            nc.scalar.dma_start(out=row[0:1, :], in_=vector.unsqueeze(0))
+            row_of[name] = row
+            if name == "bias":
+                w_planes = consts.tile([P, PASSES, H], U8, align_bytes=64)
+                nc.vector.memset(w_planes[:].bitcast(I32), 0)
+        eps = consts.tile([P, 1], F32)
+        nc.vector.memset(eps[:], EPS)
+        ident = consts.tile([P, P], F32)
+        make_identity(nc, ident[:])
+        ident_bf = consts.tile([P, P], BF16)
+        make_identity(nc, ident_bf[:])
 
-        rows = consts.tile([P, 3, H], BF16)
-        nc.vector.memset(rows[:].bitcast(I32), 0)
-        for v, vector in enumerate((ln2_g, ln2_b, b_f)):
-            nc.sync.dma_start(out=rows[0:1, v, :], in_=vector.unsqueeze(0))
-
-        w_words = consts.tile([P, PASSES, 2 * H], U8, align_bytes=64)
-        nc.sync.dma_start(
-            out=w_words[:].bitcast(I32),
-            in_=Wf_words.rearrange("g p b -> p g b").bitcast(I32),
-        )
-        w_planes = consts.tile([P, PASSES, H], U8, align_bytes=64)
-        nc.vector.memset(w_planes[:].bitcast(I32), 0)
+        load_ff(0)
         for quadrant in range(4):
             nc.sync.dma_start(
                 out=w_planes[32 * quadrant : 32 * quadrant + 4].bitcast(I32),
@@ -112,29 +149,37 @@ def tile_disentangledattention_pc_t_kernel(
                 .rearrange("g r n -> r g n")
                 .bitcast(I32),
             )
+        w_words = consts.tile([P, PASSES, 2 * H], U8, align_bytes=64)
+        nc.sync.dma_start(
+            out=w_words[:].bitcast(I32),
+            in_=Wf_words.rearrange("g p b -> p g b").bitcast(I32),
+        )
+        for t in range(first_step + FF_LEAD):
+            if t > 0:
+                load_ff(t)
+            if t < first_step + ATTN_LEAD:
+                load_attn(t)
 
-        for t in range(ATTN_LEAD - TRANSPOSE_LEAD):
-            load_attn(t)
+        bias_sb = consts.tile([P, H], BF16)
 
-        ones = consts.tile([P, P], BF16)
-        nc.vector.memset(ones[:], 1.0)
-        eps = consts.tile([P, 1], F32)
-        nc.vector.memset(eps[:], EPS)
-        ident = consts.tile([P, P], F32)
-        make_identity(nc, ident[:])
+        def spread_bias():
+            for h in range(HALVES):
+                cols = slice(h * BANK, (h + 1) * BANK)
+                acc = psum_acc.tile([P, BANK], F32)
+                nc.tensor.matmul(out=acc[:], lhsT=ones[:], rhs=row_of["bias"][:, cols], start=True, stop=True)
+                nc.scalar.copy(out=bias_sb[:, cols], in_=acc[:])
 
         gain_ps = psum_const.tile([P, H], BF16)
         shift_ps = psum_const.tile([P, H], BF16)
-        bias_sb = consts.tile([P, H], BF16)
-        for h in range(HALVES):
-            cols = slice(h * BANK, (h + 1) * BANK)
-            nc.tensor.matmul(out=gain_ps[:, cols], lhsT=ones[:], rhs=rows[:, 0, cols], start=True, stop=True)
-            nc.tensor.matmul(out=shift_ps[:, cols], lhsT=ones[:], rhs=rows[:, 1, cols], start=True, stop=True)
-            acc = psum_acc.tile([P, BANK], F32)
-            nc.tensor.matmul(out=acc[:], lhsT=ones[:], rhs=rows[:, 2, cols], start=True, stop=True)
-            nc.scalar.copy(out=bias_sb[:, cols], in_=acc[:])
         shift_sb = consts.tile([P, H], BF16)
-        nc.scalar.copy(out=shift_sb[:], in_=shift_ps[:])
+
+        def spread_gain_and_shift():
+            for h in range(HALVES):
+                cols = slice(h * BANK, (h + 1) * BANK)
+                nc.tensor.matmul(out=gain_ps[:, cols], lhsT=ones[:], rhs=row_of["gain"][:, cols], start=True, stop=True)
+            for h in range(HALVES):
+                cols = slice(h * BANK, (h + 1) * BANK)
+                nc.tensor.matmul(out=shift_ps[:, cols], lhsT=ones[:], rhs=row_of["shift"][:, cols], start=True, stop=True)
 
         def transpose(t):
             words = ff_of[t][:].bitcast(F32)
@@ -147,12 +192,11 @@ def tile_disentangledattention_pc_t_kernel(
                         ident[:],
                     )
             xt_of[t] = xt
-            load_ff(t + AHEAD)
 
         def regroup(t):
-            c, j = divmod(t, GROUP)
+            c, j = place_of[t]
             if j == 0:
-                grouped = quant.tile([P, GROUP, PASSES, P, PACK], BF16, align_bytes=64)
+                grouped = quant.tile([P, GROUP_SIZES[c], PASSES, P, PACK], BF16, align_bytes=64)
                 grouped_of[c] = grouped
             nc.scalar.copy(
                 out=grouped_of[c][:, j].bitcast(F32),
@@ -160,8 +204,8 @@ def tile_disentangledattention_pc_t_kernel(
             )
 
         def quantise(c):
-            codes = quant.tile([P, GROUP, PASSES, P], U32, align_bytes=64)
-            planes = quant.tile([P, GROUP, PASSES, P], U8, align_bytes=64)
+            codes = quant.tile([P, GROUP_SIZES[c], PASSES, P], U32, align_bytes=64)
+            planes = quant.tile([P, GROUP_SIZES[c], PASSES, P], U8, align_bytes=64)
             nc.vector.quantize_mx(
                 out=codes[:].rearrange("p j g r -> p (j g r)").bitcast(FP8X4),
                 scales=planes[:].rearrange("p j g r -> p (j g r)"),
@@ -172,9 +216,9 @@ def tile_disentangledattention_pc_t_kernel(
             gate = stats.tile([P, 1], U32)
             nc.gpsimd.tensor_copy(out=gate[:], in_=codes[:, 0, 0, 0:1])
 
-        def multiply(t):
-            c, j = divmod(t, GROUP)
-            for h in range(HALVES):
+        def multiply(t, halves=(0, 1)):
+            c, j = place_of[t]
+            for h in halves:
                 acc = psum_acc.tile([P, BANK], F32)
                 for g in range(PASSES):
                     nc.tensor.matmul_mx(
@@ -188,8 +232,28 @@ def tile_disentangledattention_pc_t_kernel(
                     )
                 acc_of[(t, h)] = acc
 
+        def on_tensor(t):
+            return TS_MOD > 0 and t % TS_MOD == TS_PHASE and t >= TS_FROM
+
+        def add_bias_on_tensor(t, h):
+            if h == 0:
+                r = resid.tile([P, H], F32)
+                r_of[t] = r
+            cols = slice(h * BANK, (h + 1) * BANK)
+            r_ps = psum_r.tile([P, BANK], F32)
+            nc.tensor.matmul(out=r_ps[:], lhsT=ones[:], rhs=row_of["bias"][:, cols], start=True, stop=False)
+            nc.tensor.matmul(out=r_ps[:], lhsT=ident_bf[:], rhs=attn_of[t][:, cols], start=False, stop=True)
+            pending.append((t, cols, r_ps))
+
+        pending = []
+
+        def evacuate():
+            for t, cols, r_ps in pending:
+                nc.scalar.copy(out=r_of[t][:, cols], in_=r_ps[:])
+            pending.clear()
+
         def add_bias(t):
-            if t >= TILES:
+            if t >= TILES or on_tensor(t):
                 return
             r = resid.tile([P, H], F32)
             nc.gpsimd.tensor_tensor(out=r[:], in0=attn_of[t][:], in1=bias_sb[:], op=ADD)
@@ -245,56 +309,82 @@ def tile_disentangledattention_pc_t_kernel(
             nc.sync.dma_start(out=out_tiles[t], in_=y[:])
 
         def shared_out(t):
-            return (t + SHIFT_LAG + QUANTISE_LEAD) % GROUP == 0
+            return t % 2 == 1 and t < TILES - 1
 
-        def scale_on_scalar_shift_on_gpsimd(t):
+        def scale_on_scalar(t):
             scaled_w = offload.tile([P, H], F32)
             nc.scalar.activation(out=scaled_w[:], in_=w_of[t][:], func=ACT.Identity, scale=rstd_of[t][:])
-            y_late = offload.tile([P, H], F32)
-            nc.gpsimd.tensor_tensor(out=y_late[:], in0=scaled_w[:], in1=shift_sb[:], op=ADD)
-            y_late_of[t] = y_late
+            scaled_w_of[t] = scaled_w
 
-        def group_due(step, lead):
-            c, j = divmod(step + lead, GROUP)
-            return c if j == 0 and 0 <= c < GROUPS else None
+        def shift_on_gpsimd(t):
+            y_late = offload.tile([P, H], F32)
+            nc.gpsimd.tensor_tensor(out=y_late[:], in0=scaled_w_of[t][:], in1=shift_sb[:], op=ADD)
+            y_late_of[t] = y_late
 
         def tile_due(step, lead):
             t = step + lead
             return t if 0 <= t < TILES else None
 
-        add_bias(0)
-        for step in range(-TRANSPOSE_LEAD, TILES + STORE_LAG):
-            t = tile_due(step, TRANSPOSE_LEAD)
-            if t is not None:
-                transpose(t)
-            t = tile_due(step, REGROUP_LEAD)
-            if t is not None:
-                regroup(t)
+        if not on_tensor(0):
+            spread_bias()
+            add_bias(0)
+        for step in range(first_step, TILES + STORE_LAG):
+            load_ff(step + FF_LEAD)
             load_attn(step + ATTN_LEAD)
+            for t in regroup_at.get(step, []):
+                regroup(t)
+            evacuate()
+            nxt = tile_due(step, MULTIPLY_LEAD)
+            if nxt is not None:
+                multiply(nxt, (0,))
+                if ORDER == 0:
+                    multiply(nxt, (1,))
+            for t in transpose_at.get(step, []):
+                transpose(t)
+            for h, lead in ((0, TS_LEAD0), (1, TS_LEAD1)):
+                t = tile_due(step, lead)
+                if t is not None and on_tensor(t):
+                    add_bias_on_tensor(t, h)
+            if nxt is not None and ORDER == 1:
+                multiply(nxt, (1,))
+            if step == SPREAD_AT:
+                spread_gain_and_shift()
+            if step == COPY_AT:
+                nc.scalar.copy(out=shift_sb[:], in_=shift_ps[:])
+            if step == first_step and on_tensor(0):
+                spread_bias()
+            last = tile_due(step, -SHIFT_LAG)
+            if last is not None and shared_out(last) and not PROD_LATE:
+                scale_on_scalar(last)
             now = tile_due(step, 0)
             if now is not None:
                 sums = add_residual(now)
-            c = group_due(step, QUANTISE_LEAD)
+            c = quantise_at.get(step)
+            sums_due = []
             if c is not None:
                 quantise(c)
-            t = tile_due(step, MULTIPLY_LEAD)
-            if t is not None:
-                multiply(t)
+                if P0_MODE == 0:
+                    sums_due = list(range(last_of[c] - GROUP_SIZES[c] + 2, last_of[c] + 2))
+            if P0_MODE == 1:
+                sums_due = [step + P0_LEAD] if step + P0_LEAD >= 1 else []
+                if step == first_step:
+                    sums_due = list(range(1, step + P0_LEAD + 1))
+            if sums_due:
+                add_bias(sums_due[0])
             if now is not None:
                 statistics(now, sums)
-            if c is not None:
-                add_bias(GROUP * c + 1)
-            t = tile_due(step, -SHIFT_LAG)
+            if last is not None and shared_out(last) and PROD_LATE:
+                scale_on_scalar(last)
+            t = tile_due(step, -LATE_SUM_LAG)
+            if t is not None and shared_out(t):
+                shift_on_gpsimd(t)
+            for t in sums_due[1:]:
+                add_bias(t)
+            t = tile_due(step, -GAIN_LAG)
             if t is not None:
-                if shared_out(t):
-                    scale_on_scalar_shift_on_gpsimd(t)
-                else:
-                    scale_shift_store(t)
-            if c is not None:
-                for j in range(2, GROUP + 1):
-                    add_bias(GROUP * c + j)
-            if now is not None:
-                centre_and_gain(now)
+                centre_and_gain(t)
+            if last is not None and not shared_out(last):
+                scale_shift_store(last)
             t = tile_due(step, -STORE_LAG)
             if t is not None and shared_out(t):
                 nc.sync.dma_start(out=out_tiles[t], in_=y_late_of[t][:])

@@ -31,6 +31,12 @@ RG_SLACK = 1
 TS_MOD = 3; TS_PHASE = 0; TS_FROM = 6
 TS_LEAD0 = 3; TS_LEAD1 = 2
 ORDER = 0
+V_FIRST = 0
+QDELAY = ()
+SEED = 0; SEED_AT = 1
+ZR = 0
+Z_LAG = 1; ZG_LAG = 2; ZST_LAG = 3
+LATE_FIRST = 0; LAST_SPLIT = 1; LAST_N = 1
 SPREAD_AT = 0; COPY_AT = 2
 ACC_BUFS = 3; XT_BUFS = 2; RP_BUFS = 1
 EVAC_LATE = 0
@@ -162,16 +168,39 @@ def tile_disentangledattention_pc_t_kernel(
 
         bias_sb = consts.tile([P, H], BF16)
 
+        bias_ps_of = {}
+        seed_t = consts.tile([P, H // P, P], F32)
+
+        def make_seed():
+            seed_ps = psum_r.tile([P, H // P, P], BF16, name="r_ps")
+            for i in range(H // P):
+                nc.tensor.transpose(seed_ps[:, i, :], bias_sb[:, i * P : (i + 1) * P], ident_bf[:])
+            nc.scalar.copy(out=seed_t[:], in_=seed_ps[:])
+
+        def first_sum_on_vector():
+            r = resid.tile([P, H], F32)
+            r_of[0] = r
+            for h in range(HALVES):
+                cols = slice(h * BANK, (h + 1) * BANK)
+                nc.vector.tensor_tensor(out=r[:, cols], in0=attn_of[0][:, cols], in1=bias_ps_of[h][:], op=ADD)
+
         def spread_bias():
             for h in range(HALVES):
                 cols = slice(h * BANK, (h + 1) * BANK)
                 acc = psum_acc.tile([P, BANK], F32)
                 nc.tensor.matmul(out=acc[:], lhsT=ones[:], rhs=row_of["bias"][:, cols], start=True, stop=True)
+                if V_FIRST == 1:
+                    if h == 0:
+                        r = resid.tile([P, H], F32)
+                        r_of[0] = r
+                    nc.vector.tensor_tensor(out=r_of[0][:, cols], in0=attn_of[0][:, cols], in1=acc[:], op=ADD)
                 nc.scalar.copy(out=bias_sb[:, cols], in_=acc[:])
+                bias_ps_of[h] = acc
 
         gain_ps = psum_const.tile([P, H], BF16)
         shift_ps = psum_const.tile([P, H], BF16)
         shift_sb = consts.tile([P, H], BF16)
+        gain_sb = consts.tile([P, H], BF16)
 
         def spread_gain_and_shift():
             for h in range(HALVES):
@@ -233,7 +262,7 @@ def tile_disentangledattention_pc_t_kernel(
                 acc_of[(t, h)] = acc
 
         def on_tensor(t):
-            return TS_MOD > 0 and t % TS_MOD == TS_PHASE and t >= TS_FROM
+            return t % 5 in (1, 3) and t >= 6
 
         def add_bias_on_tensor(t, h):
             if h == 0:
@@ -241,7 +270,14 @@ def tile_disentangledattention_pc_t_kernel(
                 r_of[t] = r
             cols = slice(h * BANK, (h + 1) * BANK)
             r_ps = psum_r.tile([P, BANK], F32)
-            nc.tensor.matmul(out=r_ps[:], lhsT=ones[:], rhs=row_of["bias"][:, cols], start=True, stop=False)
+            if SEED:
+                for q in range(4):
+                    nc.tensor.matmul(
+                        out=r_ps[:, q * P : (q + 1) * P], lhsT=seed_t[:, 4 * h + q, :], rhs=ident[:],
+                        is_transpose=True, start=(q == 0), stop=False,
+                    )
+            else:
+                nc.tensor.matmul(out=r_ps[:], lhsT=ones[:], rhs=row_of["bias"][:, cols], start=True, stop=False)
             nc.tensor.matmul(out=r_ps[:], lhsT=ident_bf[:], rhs=attn_of[t][:, cols], start=False, stop=True)
             pending.append((t, cols, r_ps))
 
@@ -303,10 +339,13 @@ def tile_disentangledattention_pc_t_kernel(
 
         def scale_shift_store(t):
             y = work.tile([P, H], F32)
-            nc.vector.scalar_tensor_tensor(
-                out=y[:], in0=w_of[t][:], scalar=rstd_of[t][:], in1=shift_ps[:], op0=MULT, op1=ADD
-            )
-            nc.sync.dma_start(out=out_tiles[t], in_=y[:])
+            pieces = LAST_SPLIT if t >= TILES - LAST_N else 1
+            for i in range(pieces):
+                cols = slice(i * H // pieces, (i + 1) * H // pieces)
+                nc.vector.scalar_tensor_tensor(
+                    out=y[:, cols], in0=w_of[t][:, cols], scalar=rstd_of[t][:], in1=shift_ps[:, cols], op0=MULT, op1=ADD
+                )
+                nc.sync.dma_start(out=out_tiles[t][:, cols], in_=y[:, cols])
 
         def shared_out(t):
             return t % 2 == 1 and t < TILES - 1
@@ -321,14 +360,35 @@ def tile_disentangledattention_pc_t_kernel(
             nc.gpsimd.tensor_tensor(out=y_late[:], in0=scaled_w_of[t][:], in1=shift_sb[:], op=ADD)
             y_late_of[t] = y_late
 
+        def z_route(t):
+            return False
+
+        def normalise_on_scalar(t):
+            shift_t = stats.tile([P, 1], F32)
+            nc.scalar.activation(out=shift_t[:], in_=negmean_of[t][:], func=ACT.Identity, scale=rstd_of[t][:])
+            z = offload.tile([P, H], F32)
+            nc.scalar.activation(out=z[:], in_=u_of[t][:], func=ACT.Identity, scale=rstd_of[t][:], bias=shift_t[:])
+            scaled_w_of[t] = z
+
+        def gain_shift_on_gpsimd(t):
+            zg = offload.tile([P, H], F32)
+            nc.gpsimd.tensor_tensor(out=zg[:], in0=scaled_w_of[t][:], in1=gain_sb[:], op=MULT)
+            y_late = offload.tile([P, H], F32)
+            nc.gpsimd.tensor_tensor(out=y_late[:], in0=zg[:], in1=shift_sb[:], op=ADD)
+            y_late_of[t] = y_late
+
         def tile_due(step, lead):
             t = step + lead
             return t if 0 <= t < TILES else None
 
         if not on_tensor(0):
             spread_bias()
-            add_bias(0)
+            if not V_FIRST:
+                add_bias(0)
         for step in range(first_step, TILES + STORE_LAG):
+            t = tile_due(step, -STORE_LAG)
+            if LATE_FIRST == 1 and t is not None and shared_out(t) and not z_route(t):
+                nc.sync.dma_start(out=out_tiles[t], in_=y_late_of[t][:])
             load_ff(step + FF_LEAD)
             load_attn(step + ATTN_LEAD)
             for t in regroup_at.get(step, []):
@@ -351,18 +411,34 @@ def tile_disentangledattention_pc_t_kernel(
                 spread_gain_and_shift()
             if step == COPY_AT:
                 nc.scalar.copy(out=shift_sb[:], in_=shift_ps[:])
+                if ZR:
+                    nc.scalar.copy(out=gain_sb[:], in_=gain_ps[:])
+            if step == SEED_AT and SEED:
+                make_seed()
             if step == first_step and on_tensor(0):
                 spread_bias()
             last = tile_due(step, -SHIFT_LAG)
+            if last is not None and z_route(last):
+                last = None
             if last is not None and shared_out(last) and not PROD_LATE:
                 scale_on_scalar(last)
+            t = tile_due(step, -Z_LAG)
+            if t is not None and z_route(t):
+                normalise_on_scalar(t)
             now = tile_due(step, 0)
             if now is not None:
                 sums = add_residual(now)
             c = quantise_at.get(step)
             sums_due = []
+            delayed = c is not None and c in QDELAY
+            if delayed:
+                t = tile_due(step, -GAIN_LAG)
+                if t is not None and not z_route(t):
+                    centre_and_gain(t)
             if c is not None:
                 quantise(c)
+                if c == 0 and V_FIRST == 2:
+                    first_sum_on_vector()
                 if P0_MODE == 0:
                     sums_due = list(range(last_of[c] - GROUP_SIZES[c] + 2, last_of[c] + 2))
             if P0_MODE == 1:
@@ -375,16 +451,24 @@ def tile_disentangledattention_pc_t_kernel(
                 statistics(now, sums)
             if last is not None and shared_out(last) and PROD_LATE:
                 scale_on_scalar(last)
+            t = tile_due(step, -ZG_LAG)
+            if t is not None and z_route(t):
+                gain_shift_on_gpsimd(t)
+            t = tile_due(step, -ZST_LAG)
+            if t is not None and z_route(t):
+                nc.sync.dma_start(out=out_tiles[t], in_=y_late_of[t][:])
             t = tile_due(step, -LATE_SUM_LAG)
-            if t is not None and shared_out(t):
+            if t is not None and shared_out(t) and not z_route(t):
                 shift_on_gpsimd(t)
+                if LATE_FIRST == 2:
+                    nc.sync.dma_start(out=out_tiles[t], in_=y_late_of[t][:])
             for t in sums_due[1:]:
                 add_bias(t)
             t = tile_due(step, -GAIN_LAG)
-            if t is not None:
+            if t is not None and not delayed and not z_route(t):
                 centre_and_gain(t)
             if last is not None and not shared_out(last):
                 scale_shift_store(last)
             t = tile_due(step, -STORE_LAG)
-            if t is not None and shared_out(t):
+            if not LATE_FIRST and t is not None and shared_out(t) and not z_route(t):
                 nc.sync.dma_start(out=out_tiles[t], in_=y_late_of[t][:])

@@ -32,7 +32,7 @@ TS_MOD = 3; TS_PHASE = 0; TS_FROM = 6
 TS_LEAD0 = 3; TS_LEAD1 = 2
 ORDER = 0
 V_FIRST = 0
-QDELAY = ()
+QDELAY = (); QRULE = 1
 SEED = 0; SEED_AT = 1
 ZR = 0
 Z_LAG = 1; ZG_LAG = 2; ZST_LAG = 3
@@ -381,6 +381,15 @@ def tile_disentangledattention_pc_t_kernel(
             t = step + lead
             return t if 0 <= t < TILES else None
 
+        crowded = set()
+        quantise_steps = sorted(quantise_at)
+        for before, after in zip(quantise_steps, quantise_steps[1:]):
+            c = quantise_at[before]
+            sums = [t for t in range(last_of[c] - GROUP_SIZES[c] + 2, last_of[c] + 2) if t < TILES and not on_tensor(t)]
+            lates = [s for s in range(before, after) if tile_due(s, -LATE_SUM_LAG) is not None and shared_out(s - LATE_SUM_LAG)]
+            if len(sums) + len(lates) > after - before:
+                crowded.add(quantise_at[after])
+
         if not on_tensor(0):
             spread_bias()
             if not V_FIRST:
@@ -430,7 +439,7 @@ def tile_disentangledattention_pc_t_kernel(
                 sums = add_residual(now)
             c = quantise_at.get(step)
             sums_due = []
-            delayed = c is not None and c in QDELAY
+            delayed = c is not None and (c in QDELAY or (QRULE and c in crowded))
             if delayed:
                 t = tile_due(step, -GAIN_LAG)
                 if t is not None and not z_route(t):

@@ -33,10 +33,11 @@ TS_LEAD0 = 3; TS_LEAD1 = 2
 ORDER = 0
 V_FIRST = 0
 QDELAY = (); QRULE = 1
-SEED = 0; SEED_AT = 1
+NV = 2; G_START = 2
+SEED = 0; SEED_AT = 1; SEED_FROM = 0
 ZR = 0
 Z_LAG = 1; ZG_LAG = 2; ZST_LAG = 3
-LATE_FIRST = 0; LAST_SPLIT = 1; LAST_N = 1
+LATE_FIRST = 2; LAST_SPLIT = 2; LAST_N = 2
 SPREAD_AT = 0; COPY_AT = 2
 ACC_BUFS = 3; XT_BUFS = 2; RP_BUFS = 1
 EVAC_LATE = 0
@@ -270,7 +271,7 @@ def tile_disentangledattention_pc_t_kernel(
                 r_of[t] = r
             cols = slice(h * BANK, (h + 1) * BANK)
             r_ps = psum_r.tile([P, BANK], F32)
-            if SEED:
+            if SEED and t >= SEED_FROM:
                 for q in range(4):
                     nc.tensor.matmul(
                         out=r_ps[:, q * P : (q + 1) * P], lhsT=seed_t[:, 4 * h + q, :], rhs=ident[:],
@@ -394,6 +395,7 @@ def tile_disentangledattention_pc_t_kernel(
             spread_bias()
             if not V_FIRST:
                 add_bias(0)
+        held = []
         for step in range(first_step, TILES + STORE_LAG):
             t = tile_due(step, -STORE_LAG)
             if LATE_FIRST == 1 and t is not None and shared_out(t) and not z_route(t):
@@ -448,8 +450,19 @@ def tile_disentangledattention_pc_t_kernel(
                 quantise(c)
                 if c == 0 and V_FIRST == 2:
                     first_sum_on_vector()
+                if c == 0 and V_FIRST == 3:
+                    for t in range(NV):
+                        r = resid.tile([P, H], F32)
+                        nc.vector.tensor_tensor(out=r[:], in0=attn_of[t][:], in1=bias_sb[:], op=ADD)
+                        r_of[t] = r
                 if P0_MODE == 0:
                     sums_due = list(range(last_of[c] - GROUP_SIZES[c] + 2, last_of[c] + 2))
+                    if V_FIRST == 3:
+                        held.extend([t for t in sums_due if t >= NV])
+                        sums_due = []
+                        if c >= G_START:
+                            sums_due = list(held)
+                            held.clear()
             if P0_MODE == 1:
                 sums_due = [step + P0_LEAD] if step + P0_LEAD >= 1 else []
                 if step == first_step:

@@ -26,25 +26,21 @@ BANK = 512
 HALVES = H // BANK
 TILES = TOKENS // P
 
-GROUP_SIZES = (1, 1, 2, 2, 2) + (4,) * 6
+GROUP_SIZES = (1, 1, 2) + (4,) * 7
 RG_SLACK = 1
-TS_MOD = 3; TS_PHASE = 0; TS_FROM = 6
-TS_LEAD0 = 3; TS_LEAD1 = 2
-ORDER = 0
-V_FIRST = 0
-QDELAY = (); QRULE = 1
-NV = 2; G_START = 2
-SEED = 0; SEED_AT = 1; SEED_FROM = 0
-ZR = 0
-Z_LAG = 1; ZG_LAG = 2; ZST_LAG = 3
-LATE_FIRST = 2; LAST_SPLIT = 2; LAST_N = 2
-SPREAD_AT = 0; COPY_AT = 2
-ACC_BUFS = 3; XT_BUFS = 2; RP_BUFS = 1
-EVAC_LATE = 0
-PROD_LATE = 0
-TS_SPLIT = 0
-P0_MODE = 0
-P0_LEAD = 3
+TS_LEAD0 = 3
+TS_LEAD1 = 2
+LAST_SPLIT = 2
+LAST_N = 2
+ACC_BUFS = 3
+XT_BUFS = 2
+RP_BUFS = 1
+SUM0_AFTER = 1
+EARLY = 8
+PACE = 2
+EARLY_SUMS = ((1,), (), (2, 3), (4, 5, 6, 7, 8))
+V_MORE = ()
+COPY_AT = 2
 assert sum(GROUP_SIZES) == TILES
 
 FLOPS = 2 * TOKENS * K * H
@@ -82,7 +78,7 @@ def tile_disentangledattention_pc_t_kernel(
         last_of[c] = first + size - 1
         for j in range(size):
             place_of[first + j] = (c, j)
-            due = first - QUANTISE_LEAD - (size - 1 - j) - (RG_SLACK if size > 2 else 0)
+            due = first - QUANTISE_LEAD - ((size - 1 - j) // (PACE if first < EARLY else 1) if size > 2 else 0) - (RG_SLACK if size > 2 and first >= EARLY else 0)
             regroup_at.setdefault(due, []).append(first + j)
             transpose_at.setdefault(due - 1, []).append(first + j)
         first += size
@@ -119,36 +115,48 @@ def tile_disentangledattention_pc_t_kernel(
         scaled_w_of = {}
 
         def load_ff(t):
-            if t < TILES:
+            if t < TILES and t not in ff_of:
                 ff_sb = ff_loads.tile([P, K], BF16)
                 nc.sync.dma_start(out=ff_sb[:], in_=ff_tiles[t])
                 ff_of[t] = ff_sb
 
         def load_attn(t):
-            if t < TILES:
+            if t < TILES and t not in attn_of:
                 attn_sb = attn_loads.tile([P, H], BF16)
                 nc.sync.dma_start(out=attn_sb[:], in_=attn_tiles[t])
                 attn_of[t] = attn_sb
 
-        ones = consts.tile([P, P], BF16)
-        nc.vector.memset(ones[:], 1.0)
         row_of = {}
-        for name, vector in (("bias", b_f), ("gain", ln2_g), ("shift", ln2_b)):
+
+        def zero_row(name, vector):
             row = consts.tile([P, H], BF16, name="row_" + name)
             nc.vector.memset(row[:].bitcast(I32), 0)
             nc.scalar.dma_start(out=row[0:1, :], in_=vector.unsqueeze(0))
             row_of[name] = row
-            if name == "bias":
-                w_planes = consts.tile([P, PASSES, H], U8, align_bytes=64)
-                nc.vector.memset(w_planes[:].bitcast(I32), 0)
+
         eps = consts.tile([P, 1], F32)
         nc.vector.memset(eps[:], EPS)
+        zero_row("bias", b_f)
+        primer = consts.tile([P, 1], F32)
+        nc.scalar.activation(out=primer[:], in_=eps[:], func=ACT.Abs_reciprocal_sqrt, bias=eps[:], scale=1.0)
+        w_planes = consts.tile([P, PASSES, H], U8, align_bytes=64)
+        nc.vector.memset(w_planes[:].bitcast(I32), 0)
+        ones = consts.tile([P, P], BF16)
+        nc.vector.memset(ones[:], 1.0)
+        zero_row("gain", ln2_g)
+        zero_row("shift", ln2_b)
         ident = consts.tile([P, P], F32)
         make_identity(nc, ident[:])
         ident_bf = consts.tile([P, P], BF16)
         make_identity(nc, ident_bf[:])
 
         load_ff(0)
+        load_ff(1)
+        w_words = consts.tile([P, PASSES, 2 * H], U8, align_bytes=64)
+        nc.sync.dma_start(
+            out=w_words[:].bitcast(I32),
+            in_=Wf_words.rearrange("g p b -> p g b").bitcast(I32),
+        )
         for quadrant in range(4):
             nc.sync.dma_start(
                 out=w_planes[32 * quadrant : 32 * quadrant + 4].bitcast(I32),
@@ -156,52 +164,31 @@ def tile_disentangledattention_pc_t_kernel(
                 .rearrange("g r n -> r g n")
                 .bitcast(I32),
             )
-        w_words = consts.tile([P, PASSES, 2 * H], U8, align_bytes=64)
-        nc.sync.dma_start(
-            out=w_words[:].bitcast(I32),
-            in_=Wf_words.rearrange("g p b -> p g b").bitcast(I32),
-        )
-        for t in range(first_step + FF_LEAD):
-            if t > 0:
-                load_ff(t)
-            if t < first_step + ATTN_LEAD:
-                load_attn(t)
+        for t in range(2):
+            load_attn(t)
 
         bias_sb = consts.tile([P, H], BF16)
 
         bias_ps_of = {}
-        seed_t = consts.tile([P, H // P, P], F32)
 
-        def make_seed():
-            seed_ps = psum_r.tile([P, H // P, P], BF16, name="r_ps")
-            for i in range(H // P):
-                nc.tensor.transpose(seed_ps[:, i, :], bias_sb[:, i * P : (i + 1) * P], ident_bf[:])
-            nc.scalar.copy(out=seed_t[:], in_=seed_ps[:])
-
-        def first_sum_on_vector():
+        def sum_on_vector(t):
             r = resid.tile([P, H], F32)
-            r_of[0] = r
+            r_of[t] = r
             for h in range(HALVES):
                 cols = slice(h * BANK, (h + 1) * BANK)
-                nc.vector.tensor_tensor(out=r[:, cols], in0=attn_of[0][:, cols], in1=bias_ps_of[h][:], op=ADD)
+                nc.vector.tensor_tensor(out=r[:, cols], in0=attn_of[t][:, cols], in1=bias_ps_of[h][:], op=ADD)
 
         def spread_bias():
             for h in range(HALVES):
                 cols = slice(h * BANK, (h + 1) * BANK)
                 acc = psum_acc.tile([P, BANK], F32)
                 nc.tensor.matmul(out=acc[:], lhsT=ones[:], rhs=row_of["bias"][:, cols], start=True, stop=True)
-                if V_FIRST == 1:
-                    if h == 0:
-                        r = resid.tile([P, H], F32)
-                        r_of[0] = r
-                    nc.vector.tensor_tensor(out=r_of[0][:, cols], in0=attn_of[0][:, cols], in1=acc[:], op=ADD)
                 nc.scalar.copy(out=bias_sb[:, cols], in_=acc[:])
                 bias_ps_of[h] = acc
 
         gain_ps = psum_const.tile([P, H], BF16)
         shift_ps = psum_const.tile([P, H], BF16)
         shift_sb = consts.tile([P, H], BF16)
-        gain_sb = consts.tile([P, H], BF16)
 
         def spread_gain_and_shift():
             for h in range(HALVES):
@@ -271,14 +258,7 @@ def tile_disentangledattention_pc_t_kernel(
                 r_of[t] = r
             cols = slice(h * BANK, (h + 1) * BANK)
             r_ps = psum_r.tile([P, BANK], F32)
-            if SEED and t >= SEED_FROM:
-                for q in range(4):
-                    nc.tensor.matmul(
-                        out=r_ps[:, q * P : (q + 1) * P], lhsT=seed_t[:, 4 * h + q, :], rhs=ident[:],
-                        is_transpose=True, start=(q == 0), stop=False,
-                    )
-            else:
-                nc.tensor.matmul(out=r_ps[:], lhsT=ones[:], rhs=row_of["bias"][:, cols], start=True, stop=False)
+            nc.tensor.matmul(out=r_ps[:], lhsT=ones[:], rhs=row_of["bias"][:, cols], start=True, stop=False)
             nc.tensor.matmul(out=r_ps[:], lhsT=ident_bf[:], rhs=attn_of[t][:, cols], start=False, stop=True)
             pending.append((t, cols, r_ps))
 
@@ -290,7 +270,7 @@ def tile_disentangledattention_pc_t_kernel(
             pending.clear()
 
         def add_bias(t):
-            if t >= TILES or on_tensor(t):
+            if t >= TILES or on_tensor(t) or t in r_of:
                 return
             r = resid.tile([P, H], F32)
             nc.gpsimd.tensor_tensor(out=r[:], in0=attn_of[t][:], in1=bias_sb[:], op=ADD)
@@ -361,23 +341,6 @@ def tile_disentangledattention_pc_t_kernel(
             nc.gpsimd.tensor_tensor(out=y_late[:], in0=scaled_w_of[t][:], in1=shift_sb[:], op=ADD)
             y_late_of[t] = y_late
 
-        def z_route(t):
-            return False
-
-        def normalise_on_scalar(t):
-            shift_t = stats.tile([P, 1], F32)
-            nc.scalar.activation(out=shift_t[:], in_=negmean_of[t][:], func=ACT.Identity, scale=rstd_of[t][:])
-            z = offload.tile([P, H], F32)
-            nc.scalar.activation(out=z[:], in_=u_of[t][:], func=ACT.Identity, scale=rstd_of[t][:], bias=shift_t[:])
-            scaled_w_of[t] = z
-
-        def gain_shift_on_gpsimd(t):
-            zg = offload.tile([P, H], F32)
-            nc.gpsimd.tensor_tensor(out=zg[:], in0=scaled_w_of[t][:], in1=gain_sb[:], op=MULT)
-            y_late = offload.tile([P, H], F32)
-            nc.gpsimd.tensor_tensor(out=y_late[:], in0=zg[:], in1=shift_sb[:], op=ADD)
-            y_late_of[t] = y_late
-
         def tile_due(step, lead):
             t = step + lead
             return t if 0 <= t < TILES else None
@@ -386,111 +349,64 @@ def tile_disentangledattention_pc_t_kernel(
         quantise_steps = sorted(quantise_at)
         for before, after in zip(quantise_steps, quantise_steps[1:]):
             c = quantise_at[before]
-            sums = [t for t in range(last_of[c] - GROUP_SIZES[c] + 2, last_of[c] + 2) if t < TILES and not on_tensor(t)]
+            sums = [t for t in (EARLY_SUMS[c] if c < len(EARLY_SUMS) else range(last_of[c] - GROUP_SIZES[c] + 2, last_of[c] + 2)) if t < TILES and not on_tensor(t)]
             lates = [s for s in range(before, after) if tile_due(s, -LATE_SUM_LAG) is not None and shared_out(s - LATE_SUM_LAG)]
             if len(sums) + len(lates) > after - before:
                 crowded.add(quantise_at[after])
 
-        if not on_tensor(0):
-            spread_bias()
-            if not V_FIRST:
-                add_bias(0)
-        held = []
         for step in range(first_step, TILES + STORE_LAG):
-            t = tile_due(step, -STORE_LAG)
-            if LATE_FIRST == 1 and t is not None and shared_out(t) and not z_route(t):
-                nc.sync.dma_start(out=out_tiles[t], in_=y_late_of[t][:])
-            load_ff(step + FF_LEAD)
-            load_attn(step + ATTN_LEAD)
+            for t in range(step + FF_LEAD + 1):
+                load_ff(t)
+                if t <= step + ATTN_LEAD:
+                    load_attn(t)
             for t in regroup_at.get(step, []):
                 regroup(t)
             evacuate()
             nxt = tile_due(step, MULTIPLY_LEAD)
             if nxt is not None:
-                multiply(nxt, (0,))
-                if ORDER == 0:
-                    multiply(nxt, (1,))
+                multiply(nxt)
             for t in transpose_at.get(step, []):
                 transpose(t)
+            if step == first_step:
+                spread_bias()
+            if step == first_step + 1:
+                spread_gain_and_shift()
             for h, lead in ((0, TS_LEAD0), (1, TS_LEAD1)):
                 t = tile_due(step, lead)
                 if t is not None and on_tensor(t):
                     add_bias_on_tensor(t, h)
-            if nxt is not None and ORDER == 1:
-                multiply(nxt, (1,))
-            if step == SPREAD_AT:
-                spread_gain_and_shift()
             if step == COPY_AT:
                 nc.scalar.copy(out=shift_sb[:], in_=shift_ps[:])
-                if ZR:
-                    nc.scalar.copy(out=gain_sb[:], in_=gain_ps[:])
-            if step == SEED_AT and SEED:
-                make_seed()
-            if step == first_step and on_tensor(0):
-                spread_bias()
             last = tile_due(step, -SHIFT_LAG)
-            if last is not None and z_route(last):
-                last = None
-            if last is not None and shared_out(last) and not PROD_LATE:
+            if last is not None and shared_out(last):
                 scale_on_scalar(last)
-            t = tile_due(step, -Z_LAG)
-            if t is not None and z_route(t):
-                normalise_on_scalar(t)
             now = tile_due(step, 0)
             if now is not None:
                 sums = add_residual(now)
             c = quantise_at.get(step)
             sums_due = []
-            delayed = c is not None and (c in QDELAY or (QRULE and c in crowded))
+            delayed = c is not None and c in crowded
             if delayed:
                 t = tile_due(step, -GAIN_LAG)
-                if t is not None and not z_route(t):
+                if t is not None:
                     centre_and_gain(t)
             if c is not None:
                 quantise(c)
-                if c == 0 and V_FIRST == 2:
-                    first_sum_on_vector()
-                if c == 0 and V_FIRST == 3:
-                    for t in range(NV):
-                        r = resid.tile([P, H], F32)
-                        nc.vector.tensor_tensor(out=r[:], in0=attn_of[t][:], in1=bias_sb[:], op=ADD)
-                        r_of[t] = r
-                if P0_MODE == 0:
-                    sums_due = list(range(last_of[c] - GROUP_SIZES[c] + 2, last_of[c] + 2))
-                    if V_FIRST == 3:
-                        held.extend([t for t in sums_due if t >= NV])
-                        sums_due = []
-                        if c >= G_START:
-                            sums_due = list(held)
-                            held.clear()
-            if P0_MODE == 1:
-                sums_due = [step + P0_LEAD] if step + P0_LEAD >= 1 else []
-                if step == first_step:
-                    sums_due = list(range(1, step + P0_LEAD + 1))
+                if c == SUM0_AFTER:
+                    sum_on_vector(0)
+                sums_due = list(EARLY_SUMS[c]) if c < len(EARLY_SUMS) else list(range(last_of[c] - GROUP_SIZES[c] + 2, last_of[c] + 2))
             if sums_due:
                 add_bias(sums_due[0])
             if now is not None:
                 statistics(now, sums)
-            if last is not None and shared_out(last) and PROD_LATE:
-                scale_on_scalar(last)
-            t = tile_due(step, -ZG_LAG)
-            if t is not None and z_route(t):
-                gain_shift_on_gpsimd(t)
-            t = tile_due(step, -ZST_LAG)
-            if t is not None and z_route(t):
-                nc.sync.dma_start(out=out_tiles[t], in_=y_late_of[t][:])
             t = tile_due(step, -LATE_SUM_LAG)
-            if t is not None and shared_out(t) and not z_route(t):
+            if t is not None and shared_out(t):
                 shift_on_gpsimd(t)
-                if LATE_FIRST == 2:
-                    nc.sync.dma_start(out=out_tiles[t], in_=y_late_of[t][:])
+                nc.sync.dma_start(out=out_tiles[t], in_=y_late_of[t][:])
             for t in sums_due[1:]:
                 add_bias(t)
             t = tile_due(step, -GAIN_LAG)
-            if t is not None and not delayed and not z_route(t):
+            if t is not None and not delayed:
                 centre_and_gain(t)
             if last is not None and not shared_out(last):
                 scale_shift_store(last)
-            t = tile_due(step, -STORE_LAG)
-            if not LATE_FIRST and t is not None and shared_out(t) and not z_route(t):
-                nc.sync.dma_start(out=out_tiles[t], in_=y_late_of[t][:])

@@ -39,7 +39,20 @@ SUM0_AFTER = 1
 EARLY = 8
 PACE = 2
 EARLY_SUMS = ((1,), (), (2, 3), (4, 5, 6, 7, 8))
-V_MORE = ()
+T_SET = tuple(range(6, TILES, 2))
+S_SET = tuple(range(1, TILES - 1, 2))
+G_SET = ()
+Z_SET = ()
+Z_LAG = 1
+ZG_LAG = 2
+ZS_LAG = 3
+SEED_STEP = -1
+SEED = 1
+MEAN_FIRST = 0
+ROOT_LATE = 1
+EVAC_FIRST = 0
+SPLIT30 = 0
+PIECES = {30: 2, 31: 2}
 COPY_AT = 2
 assert sum(GROUP_SIZES) == TILES
 
@@ -113,6 +126,10 @@ def tile_disentangledattention_pc_t_kernel(
         rstd_of = {}
         y_late_of = {}
         scaled_w_of = {}
+        ssq_of = {}
+        z_of = {}
+        zg_of = {}
+        gain_sb = consts.tile([P, H], BF16)
 
         def load_ff(t):
             if t < TILES and t not in ff_of:
@@ -170,6 +187,14 @@ def tile_disentangledattention_pc_t_kernel(
         bias_sb = consts.tile([P, H], BF16)
 
         bias_ps_of = {}
+
+        seed_t = consts.tile([P, H // P, P], F32)
+
+        def make_seed():
+            seed_ps = psum_r.tile([P, H // P, P], BF16, name="r_ps")
+            for i in range(H // P):
+                nc.tensor.transpose(seed_ps[:, i, :], bias_sb[:, i * P : (i + 1) * P], ident_bf[:])
+            nc.scalar.copy(out=seed_t[:], in_=seed_ps[:])
 
         def sum_on_vector(t):
             r = resid.tile([P, H], F32)
@@ -250,7 +275,7 @@ def tile_disentangledattention_pc_t_kernel(
                 acc_of[(t, h)] = acc
 
         def on_tensor(t):
-            return t % 5 in (1, 3) and t >= 6
+            return t in T_SET
 
         def add_bias_on_tensor(t, h):
             if h == 0:
@@ -258,7 +283,14 @@ def tile_disentangledattention_pc_t_kernel(
                 r_of[t] = r
             cols = slice(h * BANK, (h + 1) * BANK)
             r_ps = psum_r.tile([P, BANK], F32)
-            nc.tensor.matmul(out=r_ps[:], lhsT=ones[:], rhs=row_of["bias"][:, cols], start=True, stop=False)
+            if SEED:
+                for q in range(4):
+                    nc.tensor.matmul(
+                        out=r_ps[:, q * P : (q + 1) * P], lhsT=seed_t[:, 4 * h + q, :], rhs=ident[:],
+                        is_transpose=True, start=(q == 0), stop=False,
+                    )
+            else:
+                nc.tensor.matmul(out=r_ps[:], lhsT=ones[:], rhs=row_of["bias"][:, cols], start=True, stop=False)
             nc.tensor.matmul(out=r_ps[:], lhsT=ident_bf[:], rhs=attn_of[t][:, cols], start=False, stop=True)
             pending.append((t, cols, r_ps))
 
@@ -293,25 +325,35 @@ def tile_disentangledattention_pc_t_kernel(
             u_of[t] = u
             return sums
 
-        def statistics(t, sums):
+        def mean(t, sums):
             scaled = stats.tile([P, HALVES], F32)
             negmean = stats.tile([P, 1], F32)
             nc.scalar.activation(
                 out=scaled[:], in_=sums[:], func=ACT.Identity, scale=-1.0 / H, accum_out=negmean[:]
             )
+            negmean_of[t] = negmean
+
+        def statistics(t):
+            negmean = negmean_of[t]
             squares = work.tile([P, H], BF16)
             ssq = stats.tile([P, 1], F32)
             nc.scalar.activation(
                 out=squares[:], in_=u_of[t][:], func=ACT.Square, bias=negmean[:], accum_out=ssq[:]
             )
+            ssq_of[t] = ssq
+
+        def root(t):
+            if t is None or t in rstd_of:
+                return
             rstd = stats.tile([P, 1], F32)
             nc.scalar.activation(
-                out=rstd[:], in_=ssq[:], func=ACT.Abs_reciprocal_sqrt, bias=eps[:], scale=1.0 / H
+                out=rstd[:], in_=ssq_of[t][:], func=ACT.Abs_reciprocal_sqrt, bias=eps[:], scale=1.0 / H
             )
-            negmean_of[t] = negmean
             rstd_of[t] = rstd
 
         def centre_and_gain(t):
+            if t in Z_SET:
+                return
             w = work.tile([P, H], F32)
             nc.vector.scalar_tensor_tensor(
                 out=w[:], in0=u_of[t][:], scalar=negmean_of[t][:], in1=gain_ps[:], op0=ADD, op1=MULT
@@ -320,7 +362,19 @@ def tile_disentangledattention_pc_t_kernel(
 
         def scale_shift_store(t):
             y = work.tile([P, H], F32)
-            pieces = LAST_SPLIT if t >= TILES - LAST_N else 1
+            if SPLIT30 and t == TILES - 2:
+                a = SPLIT30
+                scaled_w = offload.tile([P, H], F32)
+                nc.scalar.activation(out=scaled_w[:, a:], in_=w_of[t][:, a:], func=ACT.Identity, scale=rstd_of[t][:])
+                nc.vector.scalar_tensor_tensor(
+                    out=y[:, :a], in0=w_of[t][:, :a], scalar=rstd_of[t][:], in1=shift_ps[:, :a], op0=MULT, op1=ADD
+                )
+                nc.sync.dma_start(out=out_tiles[t][:, :a], in_=y[:, :a])
+                y_late = offload.tile([P, H], F32)
+                nc.gpsimd.tensor_tensor(out=y_late[:, a:], in0=scaled_w[:, a:], in1=shift_sb[:, a:], op=ADD)
+                nc.sync.dma_start(out=out_tiles[t][:, a:], in_=y_late[:, a:])
+                return
+            pieces = PIECES.get(t, 1)
             for i in range(pieces):
                 cols = slice(i * H // pieces, (i + 1) * H // pieces)
                 nc.vector.scalar_tensor_tensor(
@@ -329,17 +383,40 @@ def tile_disentangledattention_pc_t_kernel(
                 nc.sync.dma_start(out=out_tiles[t][:, cols], in_=y[:, cols])
 
         def shared_out(t):
-            return t % 2 == 1 and t < TILES - 1
+            return t in S_SET or t in G_SET
 
         def scale_on_scalar(t):
+            if t in G_SET:
+                return
             scaled_w = offload.tile([P, H], F32)
             nc.scalar.activation(out=scaled_w[:], in_=w_of[t][:], func=ACT.Identity, scale=rstd_of[t][:])
             scaled_w_of[t] = scaled_w
 
         def shift_on_gpsimd(t):
+            if t in G_SET:
+                scaled_w = offload.tile([P, H], F32)
+                nc.gpsimd.tensor_scalar(out=scaled_w[:], in0=w_of[t][:], scalar1=rstd_of[t][:], scalar2=0.0, op0=MULT, op1=ADD)
+                scaled_w_of[t] = scaled_w
             y_late = offload.tile([P, H], F32)
             nc.gpsimd.tensor_tensor(out=y_late[:], in0=scaled_w_of[t][:], in1=shift_sb[:], op=ADD)
             y_late_of[t] = y_late
+
+        def normalise_on_scalar(t):
+            shift_t = stats.tile([P, 1], F32)
+            nc.scalar.activation(out=shift_t[:], in_=negmean_of[t][:], func=ACT.Identity, scale=rstd_of[t][:])
+            z = offload.tile([P, H], F32)
+            nc.scalar.activation(out=z[:], in_=u_of[t][:], func=ACT.Identity, scale=rstd_of[t][:], bias=shift_t[:])
+            z_of[t] = z
+
+        def gain_on_gpsimd(t):
+            zg = offload.tile([P, H], F32)
+            nc.gpsimd.tensor_tensor(out=zg[:], in0=z_of[t][:], in1=gain_sb[:], op=MULT)
+            zg_of[t] = zg
+
+        def late_shift_on_gpsimd(t):
+            y_late = offload.tile([P, H], F32)
+            nc.gpsimd.tensor_tensor(out=y_late[:], in0=zg_of[t][:], in1=shift_sb[:], op=ADD)
+            nc.sync.dma_start(out=out_tiles[t], in_=y_late[:])
 
         def tile_due(step, lead):
             t = step + lead
@@ -351,6 +428,7 @@ def tile_disentangledattention_pc_t_kernel(
             c = quantise_at[before]
             sums = [t for t in (EARLY_SUMS[c] if c < len(EARLY_SUMS) else range(last_of[c] - GROUP_SIZES[c] + 2, last_of[c] + 2)) if t < TILES and not on_tensor(t)]
             lates = [s for s in range(before, after) if tile_due(s, -LATE_SUM_LAG) is not None and shared_out(s - LATE_SUM_LAG)]
+            lates += [s for s in range(before, after) for g in (ZG_LAG, ZS_LAG) if s - g in Z_SET]
             if len(sums) + len(lates) > after - before:
                 crowded.add(quantise_at[after])
 
@@ -359,8 +437,12 @@ def tile_disentangledattention_pc_t_kernel(
                 load_ff(t)
                 if t <= step + ATTN_LEAD:
                     load_attn(t)
+            if EVAC_FIRST:
+                evacuate()
             for t in regroup_at.get(step, []):
                 regroup(t)
+            if ROOT_LATE:
+                root(tile_due(step, -1))
             evacuate()
             nxt = tile_due(step, MULTIPLY_LEAD)
             if nxt is not None:
@@ -375,14 +457,28 @@ def tile_disentangledattention_pc_t_kernel(
                 t = tile_due(step, lead)
                 if t is not None and on_tensor(t):
                     add_bias_on_tensor(t, h)
+            if step == SEED_STEP and SEED:
+                make_seed()
             if step == COPY_AT:
                 nc.scalar.copy(out=shift_sb[:], in_=shift_ps[:])
+                nc.scalar.copy(out=gain_sb[:], in_=gain_ps[:])
             last = tile_due(step, -SHIFT_LAG)
-            if last is not None and shared_out(last):
-                scale_on_scalar(last)
             now = tile_due(step, 0)
+            if not MEAN_FIRST:
+                if last is not None and shared_out(last):
+                    scale_on_scalar(last)
+                t = tile_due(step, -Z_LAG)
+                if t in Z_SET:
+                    normalise_on_scalar(t)
             if now is not None:
                 sums = add_residual(now)
+                mean(now, sums)
+            if MEAN_FIRST:
+                if last is not None and shared_out(last):
+                    scale_on_scalar(last)
+                t = tile_due(step, -Z_LAG)
+                if t in Z_SET:
+                    normalise_on_scalar(t)
             c = quantise_at.get(step)
             sums_due = []
             delayed = c is not None and c in crowded
@@ -398,7 +494,15 @@ def tile_disentangledattention_pc_t_kernel(
             if sums_due:
                 add_bias(sums_due[0])
             if now is not None:
-                statistics(now, sums)
+                statistics(now)
+                if not ROOT_LATE or now >= TILES - 1:
+                    root(now)
+            t = tile_due(step, -ZG_LAG)
+            if t in Z_SET:
+                gain_on_gpsimd(t)
+            t = tile_due(step, -ZS_LAG)
+            if t in Z_SET:
+                late_shift_on_gpsimd(t)
             t = tile_due(step, -LATE_SUM_LAG)
             if t is not None and shared_out(t):
                 shift_on_gpsimd(t)
@@ -408,5 +512,5 @@ def tile_disentangledattention_pc_t_kernel(
             t = tile_due(step, -GAIN_LAG)
             if t is not None and not delayed:
                 centre_and_gain(t)
-            if last is not None and not shared_out(last):
+            if last is not None and not shared_out(last) and last not in Z_SET:
                 scale_shift_store(last)

@@ -42,18 +42,12 @@ EARLY_SUMS = ((1,), (), (2, 3), (4, 5, 6, 7, 8))
 T_SET = tuple(range(6, TILES, 2))
 S_SET = tuple(range(1, TILES - 1, 2))
 G_SET = ()
-Z_SET = ()
-Z_LAG = 1
-ZG_LAG = 2
-ZS_LAG = 3
-SEED_STEP = -1
 SEED = 1
 MEAN_FIRST = 0
 ROOT_LATE = 1
 EVAC_FIRST = 0
 SPLIT30 = 0
 PIECES = {30: 2, 31: 2}
-COPY_AT = 2
 assert sum(GROUP_SIZES) == TILES
 
 FLOPS = 2 * TOKENS * K * H
@@ -127,9 +121,6 @@ def tile_disentangledattention_pc_t_kernel(
         y_late_of = {}
         scaled_w_of = {}
         ssq_of = {}
-        z_of = {}
-        zg_of = {}
-        gain_sb = consts.tile([P, H], BF16)
 
         def load_ff(t):
             if t < TILES and t not in ff_of:
@@ -190,11 +181,16 @@ def tile_disentangledattention_pc_t_kernel(
 
         seed_t = consts.tile([P, H // P, P], F32)
 
-        def make_seed():
+        seed_ps_of = {}
+
+        def turn_seed():
             seed_ps = psum_r.tile([P, H // P, P], BF16, name="r_ps")
             for i in range(H // P):
                 nc.tensor.transpose(seed_ps[:, i, :], bias_sb[:, i * P : (i + 1) * P], ident_bf[:])
-            nc.scalar.copy(out=seed_t[:], in_=seed_ps[:])
+            seed_ps_of[0] = seed_ps
+
+        def make_seed():
+            nc.scalar.copy(out=seed_t[:], in_=seed_ps_of[0][:])
 
         def sum_on_vector(t):
             r = resid.tile([P, H], F32)
@@ -352,8 +348,6 @@ def tile_disentangledattention_pc_t_kernel(
             rstd_of[t] = rstd
 
         def centre_and_gain(t):
-            if t in Z_SET:
-                return
             w = work.tile([P, H], F32)
             nc.vector.scalar_tensor_tensor(
                 out=w[:], in0=u_of[t][:], scalar=negmean_of[t][:], in1=gain_ps[:], op0=ADD, op1=MULT
@@ -401,23 +395,6 @@ def tile_disentangledattention_pc_t_kernel(
             nc.gpsimd.tensor_tensor(out=y_late[:], in0=scaled_w_of[t][:], in1=shift_sb[:], op=ADD)
             y_late_of[t] = y_late
 
-        def normalise_on_scalar(t):
-            shift_t = stats.tile([P, 1], F32)
-            nc.scalar.activation(out=shift_t[:], in_=negmean_of[t][:], func=ACT.Identity, scale=rstd_of[t][:])
-            z = offload.tile([P, H], F32)
-            nc.scalar.activation(out=z[:], in_=u_of[t][:], func=ACT.Identity, scale=rstd_of[t][:], bias=shift_t[:])
-            z_of[t] = z
-
-        def gain_on_gpsimd(t):
-            zg = offload.tile([P, H], F32)
-            nc.gpsimd.tensor_tensor(out=zg[:], in0=z_of[t][:], in1=gain_sb[:], op=MULT)
-            zg_of[t] = zg
-
-        def late_shift_on_gpsimd(t):
-            y_late = offload.tile([P, H], F32)
-            nc.gpsimd.tensor_tensor(out=y_late[:], in0=zg_of[t][:], in1=shift_sb[:], op=ADD)
-            nc.sync.dma_start(out=out_tiles[t], in_=y_late[:])
-
         def tile_due(step, lead):
             t = step + lead
             return t if 0 <= t < TILES else None
@@ -428,7 +405,6 @@ def tile_disentangledattention_pc_t_kernel(
             c = quantise_at[before]
             sums = [t for t in (EARLY_SUMS[c] if c < len(EARLY_SUMS) else range(last_of[c] - GROUP_SIZES[c] + 2, last_of[c] + 2)) if t < TILES and not on_tensor(t)]
             lates = [s for s in range(before, after) if tile_due(s, -LATE_SUM_LAG) is not None and shared_out(s - LATE_SUM_LAG)]
-            lates += [s for s in range(before, after) for g in (ZG_LAG, ZS_LAG) if s - g in Z_SET]
             if len(sums) + len(lates) > after - before:
                 crowded.add(quantise_at[after])
 
@@ -453,32 +429,25 @@ def tile_disentangledattention_pc_t_kernel(
                 spread_bias()
             if step == first_step + 1:
                 spread_gain_and_shift()
+                turn_seed()
+            if step == -1:
+                make_seed()
+                nc.scalar.copy(out=shift_sb[:], in_=shift_ps[:])
             for h, lead in ((0, TS_LEAD0), (1, TS_LEAD1)):
                 t = tile_due(step, lead)
                 if t is not None and on_tensor(t):
                     add_bias_on_tensor(t, h)
-            if step == SEED_STEP and SEED:
-                make_seed()
-            if step == COPY_AT:
-                nc.scalar.copy(out=shift_sb[:], in_=shift_ps[:])
-                nc.scalar.copy(out=gain_sb[:], in_=gain_ps[:])
             last = tile_due(step, -SHIFT_LAG)
             now = tile_due(step, 0)
             if not MEAN_FIRST:
                 if last is not None and shared_out(last):
                     scale_on_scalar(last)
-                t = tile_due(step, -Z_LAG)
-                if t in Z_SET:
-                    normalise_on_scalar(t)
             if now is not None:
                 sums = add_residual(now)
                 mean(now, sums)
             if MEAN_FIRST:
                 if last is not None and shared_out(last):
                     scale_on_scalar(last)
-                t = tile_due(step, -Z_LAG)
-                if t in Z_SET:
-                    normalise_on_scalar(t)
             c = quantise_at.get(step)
             sums_due = []
             delayed = c is not None and c in crowded
@@ -497,12 +466,6 @@ def tile_disentangledattention_pc_t_kernel(
                 statistics(now)
                 if not ROOT_LATE or now >= TILES - 1:
                     root(now)
-            t = tile_due(step, -ZG_LAG)
-            if t in Z_SET:
-                gain_on_gpsimd(t)
-            t = tile_due(step, -ZS_LAG)
-            if t in Z_SET:
-                late_shift_on_gpsimd(t)
             t = tile_due(step, -LATE_SUM_LAG)
             if t is not None and shared_out(t):
                 shift_on_gpsimd(t)
@@ -512,5 +475,5 @@ def tile_disentangledattention_pc_t_kernel(
             t = tile_due(step, -GAIN_LAG)
             if t is not None and not delayed:
                 centre_and_gain(t)
-            if last is not None and not shared_out(last) and last not in Z_SET:
+            if last is not None and not shared_out(last):
                 scale_shift_store(last)

@@ -28,21 +28,27 @@ TILES = TOKENS // P
 
 GROUP_SIZES = (1, 1, 2) + (4,) * 7
 RG_SLACK = 1
-TS_LEAD0 = 3
-TS_LEAD1 = 2
+TS_LEAD0 = 4
+TS_LEAD1 = 3
 LAST_SPLIT = 2
 LAST_N = 2
-ACC_BUFS = 3
+ACC_BUFS = 2
 XT_BUFS = 2
-RP_BUFS = 1
+RP_BUFS = 2
 SUM0_AFTER = 1
+SUM2 = 1
+HEAD_LOADS = 0
 EARLY = 8
 PACE = 2
-EARLY_SUMS = ((1,), (), (2, 3), (4, 5, 6, 7, 8))
-T_SET = tuple(range(6, TILES, 2))
-S_SET = tuple(range(1, TILES - 1, 2))
+EARLY_SUMS = ((1,), (), (3,), (4, 5, 6, 7, 8))
+T_SET = tuple(t for t in range(6, TILES - 1) if t % 3 != 1)
+S_SET = (28,)
 G_SET = ()
 SEED = 1
+Z_SET = tuple(range(3, 28, 3))
+Z_LAG = 1
+ZG_LAG = 2
+ZS_LAG = 3
 MEAN_FIRST = 0
 ROOT_LATE = 1
 EVAC_FIRST = 0
@@ -120,6 +126,9 @@ def tile_disentangledattention_pc_t_kernel(
         rstd_of = {}
         y_late_of = {}
         scaled_w_of = {}
+        z_of = {}
+        zg_of = {}
+        gain_sb = consts.tile([P, H], BF16)
         ssq_of = {}
 
         def load_ff(t):
@@ -172,8 +181,17 @@ def tile_disentangledattention_pc_t_kernel(
                 .rearrange("g r n -> r g n")
                 .bitcast(I32),
             )
-        for t in range(2):
-            load_attn(t)
+        load_attn(0)
+        if HEAD_LOADS == 0:
+            load_attn(1)
+        elif HEAD_LOADS == 1:
+            load_ff(2)
+            load_attn(1)
+            load_ff(3)
+        elif HEAD_LOADS == 2:
+            load_ff(2)
+            load_ff(3)
+            load_attn(1)
 
         bias_sb = consts.tile([P, H], BF16)
 
@@ -348,6 +366,8 @@ def tile_disentangledattention_pc_t_kernel(
             rstd_of[t] = rstd
 
         def centre_and_gain(t):
+            if t in Z_SET:
+                return
             w = work.tile([P, H], F32)
             nc.vector.scalar_tensor_tensor(
                 out=w[:], in0=u_of[t][:], scalar=negmean_of[t][:], in1=gain_ps[:], op0=ADD, op1=MULT
@@ -395,6 +415,23 @@ def tile_disentangledattention_pc_t_kernel(
             nc.gpsimd.tensor_tensor(out=y_late[:], in0=scaled_w_of[t][:], in1=shift_sb[:], op=ADD)
             y_late_of[t] = y_late
 
+        def normalise_on_scalar(t):
+            shift_t = stats.tile([P, 1], F32)
+            nc.scalar.activation(out=shift_t[:], in_=negmean_of[t][:], func=ACT.Identity, scale=rstd_of[t][:])
+            z = offload.tile([P, H], F32)
+            nc.scalar.activation(out=z[:], in_=u_of[t][:], func=ACT.Identity, scale=rstd_of[t][:], bias=shift_t[:])
+            z_of[t] = z
+
+        def gain_on_gpsimd(t):
+            zg = offload.tile([P, H], F32)
+            nc.gpsimd.tensor_tensor(out=zg[:], in0=z_of[t][:], in1=gain_sb[:], op=MULT)
+            zg_of[t] = zg
+
+        def late_shift_on_gpsimd(t):
+            y_late = offload.tile([P, H], F32)
+            nc.gpsimd.tensor_tensor(out=y_late[:], in0=zg_of[t][:], in1=shift_sb[:], op=ADD)
+            nc.sync.dma_start(out=out_tiles[t], in_=y_late[:])
+
         def tile_due(step, lead):
             t = step + lead
             return t if 0 <= t < TILES else None
@@ -405,6 +442,7 @@ def tile_disentangledattention_pc_t_kernel(
             c = quantise_at[before]
             sums = [t for t in (EARLY_SUMS[c] if c < len(EARLY_SUMS) else range(last_of[c] - GROUP_SIZES[c] + 2, last_of[c] + 2)) if t < TILES and not on_tensor(t)]
             lates = [s for s in range(before, after) if tile_due(s, -LATE_SUM_LAG) is not None and shared_out(s - LATE_SUM_LAG)]
+            lates += [s for s in range(before, after) for g in (ZG_LAG, ZS_LAG) if s - g in Z_SET]
             if len(sums) + len(lates) > after - before:
                 crowded.add(quantise_at[after])
 
@@ -433,6 +471,7 @@ def tile_disentangledattention_pc_t_kernel(
             if step == -1:
                 make_seed()
                 nc.scalar.copy(out=shift_sb[:], in_=shift_ps[:])
+                nc.scalar.copy(out=gain_sb[:], in_=gain_ps[:])
             for h, lead in ((0, TS_LEAD0), (1, TS_LEAD1)):
                 t = tile_due(step, lead)
                 if t is not None and on_tensor(t):
@@ -442,12 +481,18 @@ def tile_disentangledattention_pc_t_kernel(
             if not MEAN_FIRST:
                 if last is not None and shared_out(last):
                     scale_on_scalar(last)
+                t = tile_due(step, -Z_LAG)
+                if t in Z_SET:
+                    normalise_on_scalar(t)
             if now is not None:
                 sums = add_residual(now)
                 mean(now, sums)
             if MEAN_FIRST:
                 if last is not None and shared_out(last):
                     scale_on_scalar(last)
+                t = tile_due(step, -Z_LAG)
+                if t in Z_SET:
+                    normalise_on_scalar(t)
             c = quantise_at.get(step)
             sums_due = []
             delayed = c is not None and c in crowded
@@ -455,6 +500,10 @@ def tile_disentangledattention_pc_t_kernel(
                 t = tile_due(step, -GAIN_LAG)
                 if t is not None:
                     centre_and_gain(t)
+            if step == 0 and SUM2:
+                r = resid.tile([P, H], F32)
+                nc.vector.tensor_tensor(out=r[:], in0=attn_of[2][:], in1=bias_sb[:], op=ADD)
+                r_of[2] = r
             if c is not None:
                 quantise(c)
                 if c == SUM0_AFTER:
@@ -466,6 +515,12 @@ def tile_disentangledattention_pc_t_kernel(
                 statistics(now)
                 if not ROOT_LATE or now >= TILES - 1:
                     root(now)
+            t = tile_due(step, -ZG_LAG)
+            if t in Z_SET:
+                gain_on_gpsimd(t)
+            t = tile_due(step, -ZS_LAG)
+            if t in Z_SET:
+                late_shift_on_gpsimd(t)
             t = tile_due(step, -LATE_SUM_LAG)
             if t is not None and shared_out(t):
                 shift_on_gpsimd(t)
@@ -475,5 +530,5 @@ def tile_disentangledattention_pc_t_kernel(
             t = tile_due(step, -GAIN_LAG)
             if t is not None and not delayed:
                 centre_and_gain(t)
-            if last is not None and not shared_out(last):
+            if last is not None and not shared_out(last) and last not in Z_SET:
                 scale_shift_store(last)

@@ -42,17 +42,19 @@ EARLY = 8
 PACE = 2
 EARLY_SUMS = ((1,), (), (3,), (4, 5, 6, 7, 8))
 T_SET = tuple(t for t in range(6, TILES - 1) if t % 3 != 1)
-S_SET = (28,)
+S_SET = (1, 28)
 G_SET = ()
 SEED = 1
 Z_SET = tuple(range(3, 28, 3))
 Z_LAG = 1
 ZG_LAG = 2
 ZS_LAG = 3
-MEAN_FIRST = 0
+ZST = 0
+TURN_FIRST_FROM = 99
+MEAN_FIRST = 1
 ROOT_LATE = 1
-EVAC_FIRST = 0
-SPLIT30 = 0
+EV_BEFORE = 1
+SPLIT30 = 512
 PIECES = {30: 2, 31: 2}
 assert sum(GROUP_SIZES) == TILES
 
@@ -310,10 +312,9 @@ def tile_disentangledattention_pc_t_kernel(
 
         pending = []
 
-        def evacuate():
-            for t, cols, r_ps in pending:
+        def evacuate(sums):
+            for t, cols, r_ps in sums:
                 nc.scalar.copy(out=r_of[t][:, cols], in_=r_ps[:])
-            pending.clear()
 
         def add_bias(t):
             if t >= TILES or on_tensor(t) or t in r_of:
@@ -430,7 +431,7 @@ def tile_disentangledattention_pc_t_kernel(
         def late_shift_on_gpsimd(t):
             y_late = offload.tile([P, H], F32)
             nc.gpsimd.tensor_tensor(out=y_late[:], in0=zg_of[t][:], in1=shift_sb[:], op=ADD)
-            nc.sync.dma_start(out=out_tiles[t], in_=y_late[:])
+            y_late_of[t] = y_late
 
         def tile_due(step, lead):
             t = step + lead
@@ -451,18 +452,22 @@ def tile_disentangledattention_pc_t_kernel(
                 load_ff(t)
                 if t <= step + ATTN_LEAD:
                     load_attn(t)
-            if EVAC_FIRST:
-                evacuate()
+            made = list(pending)
+            pending.clear()
             for t in regroup_at.get(step, []):
                 regroup(t)
             if ROOT_LATE:
                 root(tile_due(step, -1))
-            evacuate()
+            evacuate(made[:EV_BEFORE])
             nxt = tile_due(step, MULTIPLY_LEAD)
+            if step >= TURN_FIRST_FROM:
+                for t in transpose_at.get(step, []):
+                    transpose(t)
             if nxt is not None:
                 multiply(nxt)
-            for t in transpose_at.get(step, []):
-                transpose(t)
+            if step < TURN_FIRST_FROM:
+                for t in transpose_at.get(step, []):
+                    transpose(t)
             if step == first_step:
                 spread_bias()
             if step == first_step + 1:
@@ -487,6 +492,7 @@ def tile_disentangledattention_pc_t_kernel(
             if now is not None:
                 sums = add_residual(now)
                 mean(now, sums)
+            evacuate(made[EV_BEFORE:])
             if MEAN_FIRST:
                 if last is not None and shared_out(last):
                     scale_on_scalar(last)
@@ -518,9 +524,14 @@ def tile_disentangledattention_pc_t_kernel(
             t = tile_due(step, -ZG_LAG)
             if t in Z_SET:
                 gain_on_gpsimd(t)
+            t = tile_due(step, -ZS_LAG - ZST)
+            if ZST and t in Z_SET:
+                nc.sync.dma_start(out=out_tiles[t], in_=y_late_of[t][:])
             t = tile_due(step, -ZS_LAG)
             if t in Z_SET:
                 late_shift_on_gpsimd(t)
+                if not ZST:
+                    nc.sync.dma_start(out=out_tiles[t], in_=y_late_of[t][:])
             t = tile_due(step, -LATE_SUM_LAG)
             if t is not None and shared_out(t):
                 shift_on_gpsimd(t)

@@ -24,54 +24,32 @@ K_PASS = P * PACK
 PASSES = K // K_PASS
 BANK = 512
 HALVES = H // BANK
+BLOCKS = BANK // P
 TILES = TOKENS // P
 
 GROUP_SIZES = (1, 1, 2) + (4,) * 7
-RG_SLACK = 1
-TS_LEAD0 = 4
-TS_LEAD1 = 3
-LAST_SPLIT = 2
-LAST_N = 2
-ACC_BUFS = 2
-XT_BUFS = 2
-RP_BUFS = 2
-SUM0_AFTER = 1
-SUM2 = 1
-HEAD_LOADS = 0
-EARLY = 8
-PACE = 2
-EARLY_SUMS = ((1,), (), (3,), (4, 5, 6, 7, 8))
-T_SET = tuple(t for t in range(6, TILES - 1) if t % 3 != 1)
-S_SET = (1, 28)
-G_SET = ()
-SEED = 1
-Z_SET = tuple(range(3, 28, 3))
-Z_LAG = 1
-ZG_LAG = 2
-ZS_LAG = 3
-ZST = 0
-TURN_FIRST_FROM = 99
-MEAN_FIRST = 1
-ROOT_LATE = 1
-EV_BEFORE = 1
-SPLIT30 = 512
-PIECES = {30: 2, 31: 2}
 assert sum(GROUP_SIZES) == TILES
-
-FLOPS = 2 * TOKENS * K * H
 
 FF_LEAD = 9
 ATTN_LEAD = 7
+TENSOR_SUM_LEADS = (4, 3)
 QUANTISE_LEAD = 2
 MULTIPLY_LEAD = 1
-TENSOR_SUM_LEAD = 3
 GAIN_LAG = 1
 SHIFT_LAG = 2
-LATE_SUM_LAG = 3
-STORE_LAG = 4
-FF_BUFS = 7
-ATTN_BUFS = 8
-R_BUFS = 7
+LATE_LAG = 3
+
+
+def addend_on_tensor(t):
+    return 6 <= t < TILES - 1 and t % 3 != 1
+
+
+def norm_on_scalar(t):
+    return 3 <= t < TILES - 4 and t % 3 == 0
+
+
+def shift_shared_out(t):
+    return t in (1, TILES - 4)
 
 
 def tile_disentangledattention_pc_t_kernel(
@@ -93,7 +71,13 @@ def tile_disentangledattention_pc_t_kernel(
         last_of[c] = first + size - 1
         for j in range(size):
             place_of[first + j] = (c, j)
-            due = first - QUANTISE_LEAD - ((size - 1 - j) // (PACE if first < EARLY else 1) if size > 2 else 0) - (RG_SLACK if size > 2 and first >= EARLY else 0)
+            if size < 4:
+                before = 0
+            elif first == 4:
+                before = (size - 1 - j) // 2
+            else:
+                before = size - j
+            due = first - QUANTISE_LEAD - before
             regroup_at.setdefault(due, []).append(first + j)
             transpose_at.setdefault(due - 1, []).append(first + j)
         first += size
@@ -102,17 +86,17 @@ def tile_disentangledattention_pc_t_kernel(
     with ExitStack() as ctx:
         ctx.enter_context(tc.manual_schedule())
         consts = ctx.enter_context(tc.tile_pool(name="consts", bufs=1))
-        ff_loads = ctx.enter_context(tc.tile_pool(name="ff_loads", bufs=FF_BUFS))
-        attn_loads = ctx.enter_context(tc.tile_pool(name="attn_loads", bufs=ATTN_BUFS))
-        resid = ctx.enter_context(tc.tile_pool(name="resid", bufs=R_BUFS))
-        offload = ctx.enter_context(tc.tile_pool(name="offload", bufs=3))
+        ff_loads = ctx.enter_context(tc.tile_pool(name="ff_loads", bufs=7))
+        attn_loads = ctx.enter_context(tc.tile_pool(name="attn_loads", bufs=8))
+        addends = ctx.enter_context(tc.tile_pool(name="addends", bufs=7))
         quant = ctx.enter_context(tc.tile_pool(name="quant", bufs=2))
         work = ctx.enter_context(tc.tile_pool(name="work", bufs=4))
+        offload = ctx.enter_context(tc.tile_pool(name="offload", bufs=3))
         stats = ctx.enter_context(tc.tile_pool(name="stats", bufs=6))
         psum_const = ctx.enter_context(tc.psum_pool(name="psum_const", bufs=1))
-        psum_acc = ctx.enter_context(tc.psum_pool(name="psum_acc", bufs=ACC_BUFS))
-        psum_r = ctx.enter_context(tc.psum_pool(name="psum_r", bufs=RP_BUFS))
-        psum_xt = ctx.enter_context(tc.psum_pool(name="psum_xt", bufs=XT_BUFS))
+        psum_acc = ctx.enter_context(tc.psum_pool(name="psum_acc", bufs=2))
+        psum_r = ctx.enter_context(tc.psum_pool(name="psum_r", bufs=2))
+        psum_xt = ctx.enter_context(tc.psum_pool(name="psum_xt", bufs=2))
 
         ff_of = {}
         attn_of = {}
@@ -123,15 +107,16 @@ def tile_disentangledattention_pc_t_kernel(
         acc_of = {}
         r_of = {}
         u_of = {}
-        w_of = {}
         negmean_of = {}
+        ssq_of = {}
         rstd_of = {}
-        y_late_of = {}
-        scaled_w_of = {}
+        w_of = {}
+        scaled_of = {}
+        offset_of = {}
         z_of = {}
         zg_of = {}
-        gain_sb = consts.tile([P, H], BF16)
-        ssq_of = {}
+        row_of = {}
+        bias_ps_of = {}
 
         def load_ff(t):
             if t < TILES and t not in ff_of:
@@ -144,8 +129,6 @@ def tile_disentangledattention_pc_t_kernel(
                 attn_sb = attn_loads.tile([P, H], BF16)
                 nc.sync.dma_start(out=attn_sb[:], in_=attn_tiles[t])
                 attn_of[t] = attn_sb
-
-        row_of = {}
 
         def zero_row(name, vector):
             row = consts.tile([P, H], BF16, name="row_" + name)
@@ -176,6 +159,7 @@ def tile_disentangledattention_pc_t_kernel(
             out=w_words[:].bitcast(I32),
             in_=Wf_words.rearrange("g p b -> p g b").bitcast(I32),
         )
+        load_attn(0)
         for quadrant in range(4):
             nc.sync.dma_start(
                 out=w_planes[32 * quadrant : 32 * quadrant + 4].bitcast(I32),
@@ -183,70 +167,52 @@ def tile_disentangledattention_pc_t_kernel(
                 .rearrange("g r n -> r g n")
                 .bitcast(I32),
             )
-        load_attn(0)
-        if HEAD_LOADS == 0:
-            load_attn(1)
-        elif HEAD_LOADS == 1:
-            load_ff(2)
-            load_attn(1)
-            load_ff(3)
-        elif HEAD_LOADS == 2:
-            load_ff(2)
-            load_ff(3)
-            load_attn(1)
+        load_ff(2)
+        load_attn(1)
+        load_ff(3)
 
+        gain_ps = psum_const.tile([P, H], BF16)
+        shift_ps = psum_const.tile([P, H], BF16)
+        gain_sb = consts.tile([P, H], BF16)
+        shift_sb = consts.tile([P, H], BF16)
         bias_sb = consts.tile([P, H], BF16)
+        turned_bias = consts.tile([P, H // P, P], F32)
+        turned_bias_ps = []
 
-        bias_ps_of = {}
-
-        seed_t = consts.tile([P, H // P, P], F32)
-
-        seed_ps_of = {}
-
-        def turn_seed():
-            seed_ps = psum_r.tile([P, H // P, P], BF16, name="r_ps")
-            for i in range(H // P):
-                nc.tensor.transpose(seed_ps[:, i, :], bias_sb[:, i * P : (i + 1) * P], ident_bf[:])
-            seed_ps_of[0] = seed_ps
-
-        def make_seed():
-            nc.scalar.copy(out=seed_t[:], in_=seed_ps_of[0][:])
-
-        def sum_on_vector(t):
-            r = resid.tile([P, H], F32)
-            r_of[t] = r
+        def spread(name, ps):
             for h in range(HALVES):
                 cols = slice(h * BANK, (h + 1) * BANK)
-                nc.vector.tensor_tensor(out=r[:, cols], in0=attn_of[t][:, cols], in1=bias_ps_of[h][:], op=ADD)
+                nc.tensor.matmul(out=ps[:, cols], lhsT=ones[:], rhs=row_of[name][:, cols], start=True, stop=True)
 
         def spread_bias():
             for h in range(HALVES):
                 cols = slice(h * BANK, (h + 1) * BANK)
-                acc = psum_acc.tile([P, BANK], F32)
-                nc.tensor.matmul(out=acc[:], lhsT=ones[:], rhs=row_of["bias"][:, cols], start=True, stop=True)
-                nc.scalar.copy(out=bias_sb[:, cols], in_=acc[:])
-                bias_ps_of[h] = acc
+                r_ps = psum_r.tile([P, BANK], F32)
+                nc.tensor.matmul(out=r_ps[:], lhsT=ones[:], rhs=row_of["bias"][:, cols], start=True, stop=True)
+                bias_ps_of[h] = r_ps
 
-        gain_ps = psum_const.tile([P, H], BF16)
-        shift_ps = psum_const.tile([P, H], BF16)
-        shift_sb = consts.tile([P, H], BF16)
-
-        def spread_gain_and_shift():
+        def keep_bias():
             for h in range(HALVES):
                 cols = slice(h * BANK, (h + 1) * BANK)
-                nc.tensor.matmul(out=gain_ps[:, cols], lhsT=ones[:], rhs=row_of["gain"][:, cols], start=True, stop=True)
-            for h in range(HALVES):
-                cols = slice(h * BANK, (h + 1) * BANK)
-                nc.tensor.matmul(out=shift_ps[:, cols], lhsT=ones[:], rhs=row_of["shift"][:, cols], start=True, stop=True)
+                nc.scalar.copy(out=bias_sb[:, cols], in_=bias_ps_of[h][:])
+
+        def turn_bias():
+            bias_turned = psum_r.tile([P, H // P, P], BF16, name="r_ps")
+            for i in range(H // P):
+                nc.tensor.transpose(bias_turned[:, i, :], bias_sb[:, i * P : (i + 1) * P], ident_bf[:])
+            turned_bias_ps.append(bias_turned)
+
+        def keep_turned_bias():
+            nc.scalar.copy(out=turned_bias[:], in_=turned_bias_ps[0][:])
 
         def transpose(t):
             words = ff_of[t][:].bitcast(F32)
             xt = psum_xt.tile([P, 2 * PASSES, P], F32)
             for g in range(PASSES):
-                for u in range(2):
+                for v in range(2):
                     nc.tensor.transpose(
-                        xt[:, 2 * g + u, :],
-                        words[:, 256 * g + u : 256 * (g + 1) : 2],
+                        xt[:, 2 * g + v, :],
+                        words[:, 256 * g + v : 256 * (g + 1) : 2],
                         ident[:],
                     )
             xt_of[t] = xt
@@ -258,7 +224,7 @@ def tile_disentangledattention_pc_t_kernel(
                 grouped_of[c] = grouped
             nc.scalar.copy(
                 out=grouped_of[c][:, j].bitcast(F32),
-                in_=xt_of[t][:].rearrange("p (g u) r -> p g r u", u=2),
+                in_=xt_of[t][:].rearrange("p (g v) r -> p g r v", v=2),
             )
 
         def quantise(c):
@@ -267,16 +233,16 @@ def tile_disentangledattention_pc_t_kernel(
             nc.vector.quantize_mx(
                 out=codes[:].rearrange("p j g r -> p (j g r)").bitcast(FP8X4),
                 scales=planes[:].rearrange("p j g r -> p (j g r)"),
-                in_=grouped_of[c][:].rearrange("p j g r t -> p (j g r t)"),
+                in_=grouped_of[c][:].rearrange("p j g r x -> p (j g r x)"),
             )
             codes_of[c] = codes
             planes_of[c] = planes
             gate = stats.tile([P, 1], U32)
             nc.gpsimd.tensor_copy(out=gate[:], in_=codes[:, 0, 0, 0:1])
 
-        def multiply(t, halves=(0, 1)):
+        def multiply(t):
             c, j = place_of[t]
-            for h in halves:
+            for h in range(HALVES):
                 acc = psum_acc.tile([P, BANK], F32)
                 for g in range(PASSES):
                     nc.tensor.matmul_mx(
@@ -290,40 +256,44 @@ def tile_disentangledattention_pc_t_kernel(
                     )
                 acc_of[(t, h)] = acc
 
-        def on_tensor(t):
-            return t in T_SET
+        def addend_on_vector(t):
+            r = addends.tile([P, H], F32)
+            for h in range(HALVES):
+                cols = slice(h * BANK, (h + 1) * BANK)
+                nc.vector.tensor_tensor(out=r[:, cols], in0=attn_of[t][:, cols], in1=bias_ps_of[h][:], op=ADD)
+            r_of[t] = r
 
-        def add_bias_on_tensor(t, h):
+        def addend_on_gpsimd(t):
+            if t < TILES and not addend_on_tensor(t):
+                r = addends.tile([P, H], F32)
+                nc.gpsimd.tensor_tensor(out=r[:], in0=attn_of[t][:], in1=bias_sb[:], op=ADD)
+                r_of[t] = r
+
+        def half_addend_on_tensor(t, h):
             if h == 0:
-                r = resid.tile([P, H], F32)
+                r = addends.tile([P, H], F32)
                 r_of[t] = r
             cols = slice(h * BANK, (h + 1) * BANK)
             r_ps = psum_r.tile([P, BANK], F32)
-            if SEED:
-                for q in range(4):
-                    nc.tensor.matmul(
-                        out=r_ps[:, q * P : (q + 1) * P], lhsT=seed_t[:, 4 * h + q, :], rhs=ident[:],
-                        is_transpose=True, start=(q == 0), stop=False,
-                    )
-            else:
-                nc.tensor.matmul(out=r_ps[:], lhsT=ones[:], rhs=row_of["bias"][:, cols], start=True, stop=False)
+            for q in range(BLOCKS):
+                nc.tensor.matmul(
+                    out=r_ps[:, q * P : (q + 1) * P],
+                    lhsT=turned_bias[:, BLOCKS * h + q, :],
+                    rhs=ident[:],
+                    is_transpose=True,
+                    start=(q == 0),
+                    stop=False,
+                )
             nc.tensor.matmul(out=r_ps[:], lhsT=ident_bf[:], rhs=attn_of[t][:, cols], start=False, stop=True)
-            pending.append((t, cols, r_ps))
+            in_psum.append((t, cols, r_ps))
 
-        pending = []
+        in_psum = []
 
-        def evacuate(sums):
+        def keep_addends(sums):
             for t, cols, r_ps in sums:
                 nc.scalar.copy(out=r_of[t][:, cols], in_=r_ps[:])
 
-        def add_bias(t):
-            if t >= TILES or on_tensor(t) or t in r_of:
-                return
-            r = resid.tile([P, H], F32)
-            nc.gpsimd.tensor_tensor(out=r[:], in0=attn_of[t][:], in1=bias_sb[:], op=ADD)
-            r_of[t] = r
-
-        def add_residual(t):
+        def residual_add(t):
             u = work.tile([P, H], F32)
             sums = stats.tile([P, HALVES], F32)
             for h in range(HALVES):
@@ -340,87 +310,79 @@ def tile_disentangledattention_pc_t_kernel(
             u_of[t] = u
             return sums
 
-        def mean(t, sums):
-            scaled = stats.tile([P, HALVES], F32)
+        def minus_mean(t, sums):
+            scaled_sums = stats.tile([P, HALVES], F32)
             negmean = stats.tile([P, 1], F32)
             nc.scalar.activation(
-                out=scaled[:], in_=sums[:], func=ACT.Identity, scale=-1.0 / H, accum_out=negmean[:]
+                out=scaled_sums[:], in_=sums[:], func=ACT.Identity, scale=-1.0 / H, accum_out=negmean[:]
             )
             negmean_of[t] = negmean
 
-        def statistics(t):
-            negmean = negmean_of[t]
+        def sum_of_squares(t):
             squares = work.tile([P, H], BF16)
             ssq = stats.tile([P, 1], F32)
             nc.scalar.activation(
-                out=squares[:], in_=u_of[t][:], func=ACT.Square, bias=negmean[:], accum_out=ssq[:]
+                out=squares[:], in_=u_of[t][:], func=ACT.Square, bias=negmean_of[t][:], accum_out=ssq[:]
             )
             ssq_of[t] = ssq
 
-        def root(t):
-            if t is None or t in rstd_of:
-                return
+        def one_over_std(t):
             rstd = stats.tile([P, 1], F32)
             nc.scalar.activation(
                 out=rstd[:], in_=ssq_of[t][:], func=ACT.Abs_reciprocal_sqrt, bias=eps[:], scale=1.0 / H
             )
             rstd_of[t] = rstd
 
-        def centre_and_gain(t):
-            if t in Z_SET:
-                return
+        def gain_step(t):
             w = work.tile([P, H], F32)
             nc.vector.scalar_tensor_tensor(
                 out=w[:], in0=u_of[t][:], scalar=negmean_of[t][:], in1=gain_ps[:], op0=ADD, op1=MULT
             )
             w_of[t] = w
 
-        def scale_shift_store(t):
-            y = work.tile([P, H], F32)
-            if SPLIT30 and t == TILES - 2:
-                a = SPLIT30
-                scaled_w = offload.tile([P, H], F32)
-                nc.scalar.activation(out=scaled_w[:, a:], in_=w_of[t][:, a:], func=ACT.Identity, scale=rstd_of[t][:])
-                nc.vector.scalar_tensor_tensor(
-                    out=y[:, :a], in0=w_of[t][:, :a], scalar=rstd_of[t][:], in1=shift_ps[:, :a], op0=MULT, op1=ADD
-                )
-                nc.sync.dma_start(out=out_tiles[t][:, :a], in_=y[:, :a])
-                y_late = offload.tile([P, H], F32)
-                nc.gpsimd.tensor_tensor(out=y_late[:, a:], in0=scaled_w[:, a:], in1=shift_sb[:, a:], op=ADD)
-                nc.sync.dma_start(out=out_tiles[t][:, a:], in_=y_late[:, a:])
-                return
-            pieces = PIECES.get(t, 1)
-            for i in range(pieces):
-                cols = slice(i * H // pieces, (i + 1) * H // pieces)
-                nc.vector.scalar_tensor_tensor(
-                    out=y[:, cols], in0=w_of[t][:, cols], scalar=rstd_of[t][:], in1=shift_ps[:, cols], op0=MULT, op1=ADD
-                )
-                nc.sync.dma_start(out=out_tiles[t][:, cols], in_=y[:, cols])
+        def shift_step(t, begin, end, y):
+            cols = slice(begin, end)
+            nc.vector.scalar_tensor_tensor(
+                out=y[:, cols], in0=w_of[t][:, cols], scalar=rstd_of[t][:], in1=shift_ps[:, cols], op0=MULT, op1=ADD
+            )
+            nc.sync.dma_start(out=out_tiles[t][:, cols], in_=y[:, cols])
 
-        def shared_out(t):
-            return t in S_SET or t in G_SET
-
-        def scale_on_scalar(t):
-            if t in G_SET:
-                return
+        def scale_on_scalar(t, begin):
             scaled_w = offload.tile([P, H], F32)
-            nc.scalar.activation(out=scaled_w[:], in_=w_of[t][:], func=ACT.Identity, scale=rstd_of[t][:])
-            scaled_w_of[t] = scaled_w
+            nc.scalar.activation(
+                out=scaled_w[:, begin:], in_=w_of[t][:, begin:], func=ACT.Identity, scale=rstd_of[t][:]
+            )
+            scaled_of[t] = scaled_w
 
-        def shift_on_gpsimd(t):
-            if t in G_SET:
-                scaled_w = offload.tile([P, H], F32)
-                nc.gpsimd.tensor_scalar(out=scaled_w[:], in0=w_of[t][:], scalar1=rstd_of[t][:], scalar2=0.0, op0=MULT, op1=ADD)
-                scaled_w_of[t] = scaled_w
+        def shift_on_gpsimd(t, begin):
             y_late = offload.tile([P, H], F32)
-            nc.gpsimd.tensor_tensor(out=y_late[:], in0=scaled_w_of[t][:], in1=shift_sb[:], op=ADD)
-            y_late_of[t] = y_late
+            nc.gpsimd.tensor_tensor(
+                out=y_late[:, begin:], in0=scaled_of[t][:, begin:], in1=shift_sb[:, begin:], op=ADD
+            )
+            nc.sync.dma_start(out=out_tiles[t][:, begin:], in_=y_late[:, begin:])
 
-        def normalise_on_scalar(t):
-            shift_t = stats.tile([P, 1], F32)
-            nc.scalar.activation(out=shift_t[:], in_=negmean_of[t][:], func=ACT.Identity, scale=rstd_of[t][:])
+        def shift_and_store(t):
+            y = work.tile([P, H], F32)
+            if t == TILES - 2:
+                scale_on_scalar(t, BANK)
+                shift_step(t, 0, BANK, y)
+                shift_on_gpsimd(t, BANK)
+            elif t == TILES - 1:
+                shift_step(t, 0, BANK, y)
+                shift_step(t, BANK, H, y)
+            else:
+                shift_step(t, 0, H, y)
+
+        def norm_offset(t):
+            offset = stats.tile([P, 1], F32)
+            nc.scalar.activation(out=offset[:], in_=negmean_of[t][:], func=ACT.Identity, scale=rstd_of[t][:])
+            offset_of[t] = offset
+
+        def norm(t):
             z = offload.tile([P, H], F32)
-            nc.scalar.activation(out=z[:], in_=u_of[t][:], func=ACT.Identity, scale=rstd_of[t][:], bias=shift_t[:])
+            nc.scalar.activation(
+                out=z[:], in_=u_of[t][:], func=ACT.Identity, scale=rstd_of[t][:], bias=offset_of[t][:]
+            )
             z_of[t] = z
 
         def gain_on_gpsimd(t):
@@ -428,118 +390,93 @@ def tile_disentangledattention_pc_t_kernel(
             nc.gpsimd.tensor_tensor(out=zg[:], in0=z_of[t][:], in1=gain_sb[:], op=MULT)
             zg_of[t] = zg
 
-        def late_shift_on_gpsimd(t):
+        def last_shift_on_gpsimd(t):
             y_late = offload.tile([P, H], F32)
             nc.gpsimd.tensor_tensor(out=y_late[:], in0=zg_of[t][:], in1=shift_sb[:], op=ADD)
-            y_late_of[t] = y_late
+            nc.sync.dma_start(out=out_tiles[t], in_=y_late[:])
 
-        def tile_due(step, lead):
-            t = step + lead
-            return t if 0 <= t < TILES else None
+        def tile_at(step):
+            return step if 0 <= step < TILES else None
 
-        crowded = set()
-        quantise_steps = sorted(quantise_at)
-        for before, after in zip(quantise_steps, quantise_steps[1:]):
-            c = quantise_at[before]
-            sums = [t for t in (EARLY_SUMS[c] if c < len(EARLY_SUMS) else range(last_of[c] - GROUP_SIZES[c] + 2, last_of[c] + 2)) if t < TILES and not on_tensor(t)]
-            lates = [s for s in range(before, after) if tile_due(s, -LATE_SUM_LAG) is not None and shared_out(s - LATE_SUM_LAG)]
-            lates += [s for s in range(before, after) for g in (ZG_LAG, ZS_LAG) if s - g in Z_SET]
-            if len(sums) + len(lates) > after - before:
-                crowded.add(quantise_at[after])
-
-        for step in range(first_step, TILES + STORE_LAG):
+        addends_until = 1
+        for step in range(first_step, TILES + LATE_LAG + 1):
             for t in range(step + FF_LEAD + 1):
                 load_ff(t)
                 if t <= step + ATTN_LEAD:
                     load_attn(t)
-            made = list(pending)
-            pending.clear()
+            now = tile_at(step)
+            nxt = tile_at(step + MULTIPLY_LEAD)
+            previous = tile_at(step - GAIN_LAG)
+            last = tile_at(step - SHIFT_LAG)
+            late = tile_at(step - LATE_LAG)
+            c = quantise_at.get(step)
+
+            made = list(in_psum)
+            in_psum.clear()
             for t in regroup_at.get(step, []):
                 regroup(t)
-            if ROOT_LATE:
-                root(tile_due(step, -1))
-            evacuate(made[:EV_BEFORE])
-            nxt = tile_due(step, MULTIPLY_LEAD)
-            if step >= TURN_FIRST_FROM:
-                for t in transpose_at.get(step, []):
-                    transpose(t)
+            if previous is not None and previous < TILES - 1:
+                one_over_std(previous)
+            keep_addends(made[:1])
+
             if nxt is not None:
                 multiply(nxt)
-            if step < TURN_FIRST_FROM:
-                for t in transpose_at.get(step, []):
-                    transpose(t)
+            for t in transpose_at.get(step, []):
+                transpose(t)
             if step == first_step:
                 spread_bias()
             if step == first_step + 1:
-                spread_gain_and_shift()
-                turn_seed()
+                keep_bias()
+                spread("gain", gain_ps)
             if step == -1:
-                make_seed()
-                nc.scalar.copy(out=shift_sb[:], in_=shift_ps[:])
+                spread("shift", shift_ps)
+                turn_bias()
                 nc.scalar.copy(out=gain_sb[:], in_=gain_ps[:])
-            for h, lead in ((0, TS_LEAD0), (1, TS_LEAD1)):
-                t = tile_due(step, lead)
-                if t is not None and on_tensor(t):
-                    add_bias_on_tensor(t, h)
-            last = tile_due(step, -SHIFT_LAG)
-            now = tile_due(step, 0)
-            if not MEAN_FIRST:
-                if last is not None and shared_out(last):
-                    scale_on_scalar(last)
-                t = tile_due(step, -Z_LAG)
-                if t in Z_SET:
-                    normalise_on_scalar(t)
+            for h, lead in enumerate(TENSOR_SUM_LEADS):
+                t = tile_at(step + lead)
+                if t is not None and addend_on_tensor(t):
+                    half_addend_on_tensor(t, h)
+
+            if previous is not None and norm_on_scalar(previous):
+                norm_offset(previous)
             if now is not None:
-                sums = add_residual(now)
-                mean(now, sums)
-            evacuate(made[EV_BEFORE:])
-            if MEAN_FIRST:
-                if last is not None and shared_out(last):
-                    scale_on_scalar(last)
-                t = tile_due(step, -Z_LAG)
-                if t in Z_SET:
-                    normalise_on_scalar(t)
-            c = quantise_at.get(step)
-            sums_due = []
-            delayed = c is not None and c in crowded
-            if delayed:
-                t = tile_due(step, -GAIN_LAG)
-                if t is not None:
-                    centre_and_gain(t)
-            if step == 0 and SUM2:
-                r = resid.tile([P, H], F32)
-                nc.vector.tensor_tensor(out=r[:], in0=attn_of[2][:], in1=bias_sb[:], op=ADD)
-                r_of[2] = r
+                minus_mean(now, residual_add(now))
+            keep_addends(made[1:])
+            if last is not None and shift_shared_out(last):
+                scale_on_scalar(last, 0)
+            if previous is not None and norm_on_scalar(previous):
+                norm(previous)
+
+            gain_first = c == 4
+            if gain_first and not norm_on_scalar(previous):
+                gain_step(previous)
+            if step == 1:
+                nc.vector.tensor_copy(out=shift_sb[:], in_=shift_ps[:])
+            due = range(0)
             if c is not None:
                 quantise(c)
-                if c == SUM0_AFTER:
-                    sum_on_vector(0)
-                sums_due = list(EARLY_SUMS[c]) if c < len(EARLY_SUMS) else list(range(last_of[c] - GROUP_SIZES[c] + 2, last_of[c] + 2))
-            if sums_due:
-                add_bias(sums_due[0])
+                if c == 0:
+                    addend_on_vector(0)
+                until = last_of[c] + (1 if c in (1, 2) else 2)
+                due = range(addends_until, until)
+                addends_until = until
+            for t in due[:1]:
+                addend_on_gpsimd(t)
             if now is not None:
-                statistics(now)
-                if not ROOT_LATE or now >= TILES - 1:
-                    root(now)
-            t = tile_due(step, -ZG_LAG)
-            if t in Z_SET:
-                gain_on_gpsimd(t)
-            t = tile_due(step, -ZS_LAG - ZST)
-            if ZST and t in Z_SET:
-                nc.sync.dma_start(out=out_tiles[t], in_=y_late_of[t][:])
-            t = tile_due(step, -ZS_LAG)
-            if t in Z_SET:
-                late_shift_on_gpsimd(t)
-                if not ZST:
-                    nc.sync.dma_start(out=out_tiles[t], in_=y_late_of[t][:])
-            t = tile_due(step, -LATE_SUM_LAG)
-            if t is not None and shared_out(t):
-                shift_on_gpsimd(t)
-                nc.sync.dma_start(out=out_tiles[t], in_=y_late_of[t][:])
-            for t in sums_due[1:]:
-                add_bias(t)
-            t = tile_due(step, -GAIN_LAG)
-            if t is not None and not delayed:
-                centre_and_gain(t)
-            if last is not None and not shared_out(last) and last not in Z_SET:
-                scale_shift_store(last)
+                sum_of_squares(now)
+                if now == TILES - 1:
+                    one_over_std(now)
+            if step == 0:
+                keep_turned_bias()
+            if last is not None and norm_on_scalar(last):
+                gain_on_gpsimd(last)
+            if late is not None and norm_on_scalar(late):
+                last_shift_on_gpsimd(late)
+            if late is not None and shift_shared_out(late):
+                shift_on_gpsimd(late, 0)
+            for t in due[1:]:
+                addend_on_gpsimd(t)
+            if previous is not None and not norm_on_scalar(previous) and not gain_first:
+                gain_step(previous)
+            if last is not None and not norm_on_scalar(last) and not shift_shared_out(last):
+                shift_and_store(last)

from contextlib import ExitStack

import concourse.mybir as mybir
from concourse.masks import make_identity

F32 = mybir.dt.float32
BF16 = mybir.dt.bfloat16
I32 = mybir.dt.int32
U32 = mybir.dt.uint32
U8 = mybir.dt.uint8
FP8X4 = mybir.dt.float8_e4m3fn_x4
FP4X4 = mybir.dt.float4_e2m1fn_x4
ADD = mybir.AluOpType.add
MULT = mybir.AluOpType.mult
ACT = mybir.ActivationFunctionType

P = 128
TOKENS = 8 * 512
K = 1024
H = 1024
EPS = 1e-7
PACK = 4
K_PASS = P * PACK
PASSES = K // K_PASS
BANK = 512
HALVES = H // BANK
BLOCKS = BANK // P
TILES = TOKENS // P

GROUP_SIZES = (1, 1, 2) + (4,) * 7
assert sum(GROUP_SIZES) == TILES

FF_LEAD = 9
ATTN_LEAD = 7
TENSOR_SUM_LEADS = (4, 3)
QUANTISE_LEAD = 2
MULTIPLY_LEAD = 1
GAIN_LAG = 1
SHIFT_LAG = 2
LATE_LAG = 3


def addend_on_tensor(t):
    return 6 <= t < TILES - 1 and t % 3 != 1


def norm_on_scalar(t):
    return 3 <= t < TILES - 4 and t % 3 == 0


def shift_shared_out(t):
    return t in (1, TILES - 4)


def tile_disentangledattention_pc_t_kernel(
    tc, ff, attn_out, Wf_words, Wf_scales, b_f, ln2_g, ln2_b, out
):
    nc = tc.nc
    ff_tiles = ff.flatten_outer_dims().rearrange("(t p) k -> t p k", p=P)
    attn_tiles = attn_out.flatten_outer_dims().rearrange("(t p) n -> t p n", p=P)
    out_tiles = out.flatten_outer_dims().rearrange("(t p) n -> t p n", p=P)

    place_of = {}
    last_of = {}
    quantise_at = {}
    regroup_at = {}
    transpose_at = {}
    first = 0
    for c, size in enumerate(GROUP_SIZES):
        quantise_at[first - QUANTISE_LEAD] = c
        last_of[c] = first + size - 1
        for j in range(size):
            place_of[first + j] = (c, j)
            if size < 4:
                before = 0
            elif first == 4:
                before = (size - 1 - j) // 2
            else:
                before = size - j
            due = first - QUANTISE_LEAD - before
            regroup_at.setdefault(due, []).append(first + j)
            transpose_at.setdefault(due - 1, []).append(first + j)
        first += size
    first_step = min(transpose_at)

    with ExitStack() as ctx:
        ctx.enter_context(tc.manual_schedule())
        consts = ctx.enter_context(tc.tile_pool(name="consts", bufs=1))
        ff_loads = ctx.enter_context(tc.tile_pool(name="ff_loads", bufs=7))
        attn_loads = ctx.enter_context(tc.tile_pool(name="attn_loads", bufs=8))
        addends = ctx.enter_context(tc.tile_pool(name="addends", bufs=7))
        quant = ctx.enter_context(tc.tile_pool(name="quant", bufs=2))
        work = ctx.enter_context(tc.tile_pool(name="work", bufs=4))
        offload = ctx.enter_context(tc.tile_pool(name="offload", bufs=3))
        stats = ctx.enter_context(tc.tile_pool(name="stats", bufs=6))
        psum_const = ctx.enter_context(tc.psum_pool(name="psum_const", bufs=1))
        psum_acc = ctx.enter_context(tc.psum_pool(name="psum_acc", bufs=2))
        psum_r = ctx.enter_context(tc.psum_pool(name="psum_r", bufs=2))
        psum_xt = ctx.enter_context(tc.psum_pool(name="psum_xt", bufs=2))

        ff_of = {}
        attn_of = {}
        xt_of = {}
        grouped_of = {}
        codes_of = {}
        planes_of = {}
        acc_of = {}
        r_of = {}
        u_of = {}
        negmean_of = {}
        ssq_of = {}
        rstd_of = {}
        w_of = {}
        scaled_of = {}
        offset_of = {}
        z_of = {}
        zg_of = {}
        row_of = {}
        bias_ps_of = {}

        def load_ff(t):
            if t < TILES and t not in ff_of:
                ff_sb = ff_loads.tile([P, K], BF16)
                nc.sync.dma_start(out=ff_sb[:], in_=ff_tiles[t])
                ff_of[t] = ff_sb

        def load_attn(t):
            if t < TILES and t not in attn_of:
                attn_sb = attn_loads.tile([P, H], BF16)
                nc.sync.dma_start(out=attn_sb[:], in_=attn_tiles[t])
                attn_of[t] = attn_sb

        def zero_row(name, vector):
            row = consts.tile([P, H], BF16, name="row_" + name)
            nc.vector.memset(row[:].bitcast(I32), 0)
            nc.scalar.dma_start(out=row[0:1, :], in_=vector.unsqueeze(0))
            row_of[name] = row

        eps = consts.tile([P, 1], F32)
        nc.vector.memset(eps[:], EPS)
        zero_row("bias", b_f)
        primer = consts.tile([P, 1], F32)
        nc.scalar.activation(out=primer[:], in_=eps[:], func=ACT.Abs_reciprocal_sqrt, bias=eps[:], scale=1.0)
        w_planes = consts.tile([P, PASSES, H], U8, align_bytes=64)
        nc.vector.memset(w_planes[:].bitcast(I32), 0)
        ones = consts.tile([P, P], BF16)
        nc.vector.memset(ones[:], 1.0)
        zero_row("gain", ln2_g)
        zero_row("shift", ln2_b)
        ident = consts.tile([P, P], F32)
        make_identity(nc, ident[:])
        ident_bf = consts.tile([P, P], BF16)
        make_identity(nc, ident_bf[:])

        load_ff(0)
        load_ff(1)
        w_words = consts.tile([P, PASSES, 2 * H], U8, align_bytes=64)
        nc.sync.dma_start(
            out=w_words[:].bitcast(I32),
            in_=Wf_words.rearrange("g p b -> p g b").bitcast(I32),
        )
        load_attn(0)
        for quadrant in range(4):
            nc.sync.dma_start(
                out=w_planes[32 * quadrant : 32 * quadrant + 4].bitcast(I32),
                in_=Wf_scales[:, 4 * quadrant : 4 * quadrant + 4, :]
                .rearrange("g r n -> r g n")
                .bitcast(I32),
            )
        load_ff(2)
        load_attn(1)
        load_ff(3)

        gain_ps = psum_const.tile([P, H], BF16)
        shift_ps = psum_const.tile([P, H], BF16)
        gain_sb = consts.tile([P, H], BF16)
        shift_sb = consts.tile([P, H], BF16)
        bias_sb = consts.tile([P, H], BF16)
        turned_bias = consts.tile([P, H // P, P], F32)
        turned_bias_ps = []

        def spread(name, ps):
            for h in range(HALVES):
                cols = slice(h * BANK, (h + 1) * BANK)
                nc.tensor.matmul(out=ps[:, cols], lhsT=ones[:], rhs=row_of[name][:, cols], start=True, stop=True)

        def spread_bias():
            for h in range(HALVES):
                cols = slice(h * BANK, (h + 1) * BANK)
                r_ps = psum_r.tile([P, BANK], F32)
                nc.tensor.matmul(out=r_ps[:], lhsT=ones[:], rhs=row_of["bias"][:, cols], start=True, stop=True)
                bias_ps_of[h] = r_ps

        def keep_bias():
            for h in range(HALVES):
                cols = slice(h * BANK, (h + 1) * BANK)
                nc.scalar.copy(out=bias_sb[:, cols], in_=bias_ps_of[h][:])

        def turn_bias():
            bias_turned = psum_r.tile([P, H // P, P], BF16, name="r_ps")
            for i in range(H // P):
                nc.tensor.transpose(bias_turned[:, i, :], bias_sb[:, i * P : (i + 1) * P], ident_bf[:])
            turned_bias_ps.append(bias_turned)

        def keep_turned_bias():
            nc.scalar.copy(out=turned_bias[:], in_=turned_bias_ps[0][:])

        def transpose(t):
            words = ff_of[t][:].bitcast(F32)
            xt = psum_xt.tile([P, 2 * PASSES, P], F32)
            for g in range(PASSES):
                for v in range(2):
                    nc.tensor.transpose(
                        xt[:, 2 * g + v, :],
                        words[:, 256 * g + v : 256 * (g + 1) : 2],
                        ident[:],
                    )
            xt_of[t] = xt

        def regroup(t):
            c, j = place_of[t]
            if j == 0:
                grouped = quant.tile([P, GROUP_SIZES[c], PASSES, P, PACK], BF16, align_bytes=64)
                grouped_of[c] = grouped
            nc.scalar.copy(
                out=grouped_of[c][:, j].bitcast(F32),
                in_=xt_of[t][:].rearrange("p (g v) r -> p g r v", v=2),
            )

        def quantise(c):
            codes = quant.tile([P, GROUP_SIZES[c], PASSES, P], U32, align_bytes=64)
            planes = quant.tile([P, GROUP_SIZES[c], PASSES, P], U8, align_bytes=64)
            nc.vector.quantize_mx(
                out=codes[:].rearrange("p j g r -> p (j g r)").bitcast(FP8X4),
                scales=planes[:].rearrange("p j g r -> p (j g r)"),
                in_=grouped_of[c][:].rearrange("p j g r x -> p (j g r x)"),
            )
            codes_of[c] = codes
            planes_of[c] = planes
            gate = stats.tile([P, 1], U32)
            nc.gpsimd.tensor_copy(out=gate[:], in_=codes[:, 0, 0, 0:1])

        def multiply(t):
            c, j = place_of[t]
            for h in range(HALVES):
                acc = psum_acc.tile([P, BANK], F32)
                for g in range(PASSES):
                    nc.tensor.matmul_mx(
                        out=acc[:],
                        lhsT=codes_of[c][:, j, g, :].bitcast(FP8X4),
                        lhsT_scale=planes_of[c][:, j, g, :],
                        rhs=w_words[:, g, 2 * h * BANK : 2 * (h + 1) * BANK].bitcast(FP4X4),
                        rhs_scale=w_planes[:, g, h * BANK : (h + 1) * BANK],
                        start=(g == 0),
                        stop=(g == PASSES - 1),
                    )
                acc_of[(t, h)] = acc

        def addend_on_vector(t):
            r = addends.tile([P, H], F32)
            for h in range(HALVES):
                cols = slice(h * BANK, (h + 1) * BANK)
                nc.vector.tensor_tensor(out=r[:, cols], in0=attn_of[t][:, cols], in1=bias_ps_of[h][:], op=ADD)
            r_of[t] = r

        def addend_on_gpsimd(t):
            if t < TILES and not addend_on_tensor(t):
                r = addends.tile([P, H], F32)
                nc.gpsimd.tensor_tensor(out=r[:], in0=attn_of[t][:], in1=bias_sb[:], op=ADD)
                r_of[t] = r

        def half_addend_on_tensor(t, h):
            if h == 0:
                r = addends.tile([P, H], F32)
                r_of[t] = r
            cols = slice(h * BANK, (h + 1) * BANK)
            r_ps = psum_r.tile([P, BANK], F32)
            for q in range(BLOCKS):
                nc.tensor.matmul(
                    out=r_ps[:, q * P : (q + 1) * P],
                    lhsT=turned_bias[:, BLOCKS * h + q, :],
                    rhs=ident[:],
                    is_transpose=True,
                    start=(q == 0),
                    stop=False,
                )
            nc.tensor.matmul(out=r_ps[:], lhsT=ident_bf[:], rhs=attn_of[t][:, cols], start=False, stop=True)
            in_psum.append((t, cols, r_ps))

        in_psum = []

        def keep_addends(sums):
            for t, cols, r_ps in sums:
                nc.scalar.copy(out=r_of[t][:, cols], in_=r_ps[:])

        def residual_add(t):
            u = work.tile([P, H], F32)
            sums = stats.tile([P, HALVES], F32)
            for h in range(HALVES):
                cols = slice(h * BANK, (h + 1) * BANK)
                nc.vector.scalar_tensor_tensor(
                    out=u[:, cols],
                    in0=acc_of[(t, h)][:],
                    scalar=0.0,
                    in1=r_of[t][:, cols],
                    op0=ADD,
                    op1=ADD,
                    accum_out=sums[:, h : h + 1],
                )
            u_of[t] = u
            return sums

        def minus_mean(t, sums):
            scaled_sums = stats.tile([P, HALVES], F32)
            negmean = stats.tile([P, 1], F32)
            nc.scalar.activation(
                out=scaled_sums[:], in_=sums[:], func=ACT.Identity, scale=-1.0 / H, accum_out=negmean[:]
            )
            negmean_of[t] = negmean

        def sum_of_squares(t):
            squares = work.tile([P, H], BF16)
            ssq = stats.tile([P, 1], F32)
            nc.scalar.activation(
                out=squares[:], in_=u_of[t][:], func=ACT.Square, bias=negmean_of[t][:], accum_out=ssq[:]
            )
            ssq_of[t] = ssq

        def one_over_std(t):
            rstd = stats.tile([P, 1], F32)
            nc.scalar.activation(
                out=rstd[:], in_=ssq_of[t][:], func=ACT.Abs_reciprocal_sqrt, bias=eps[:], scale=1.0 / H
            )
            rstd_of[t] = rstd

        def gain_step(t):
            w = work.tile([P, H], F32)
            nc.vector.scalar_tensor_tensor(
                out=w[:], in0=u_of[t][:], scalar=negmean_of[t][:], in1=gain_ps[:], op0=ADD, op1=MULT
            )
            w_of[t] = w

        def shift_step(t, begin, end, y):
            cols = slice(begin, end)
            nc.vector.scalar_tensor_tensor(
                out=y[:, cols], in0=w_of[t][:, cols], scalar=rstd_of[t][:], in1=shift_ps[:, cols], op0=MULT, op1=ADD
            )
            nc.sync.dma_start(out=out_tiles[t][:, cols], in_=y[:, cols])

        def scale_on_scalar(t, begin):
            scaled_w = offload.tile([P, H], F32)
            nc.scalar.activation(
                out=scaled_w[:, begin:], in_=w_of[t][:, begin:], func=ACT.Identity, scale=rstd_of[t][:]
            )
            scaled_of[t] = scaled_w

        def shift_on_gpsimd(t, begin):
            y_late = offload.tile([P, H], F32)
            nc.gpsimd.tensor_tensor(
                out=y_late[:, begin:], in0=scaled_of[t][:, begin:], in1=shift_sb[:, begin:], op=ADD
            )
            nc.sync.dma_start(out=out_tiles[t][:, begin:], in_=y_late[:, begin:])

        def shift_and_store(t):
            y = work.tile([P, H], F32)
            if t == TILES - 2:
                scale_on_scalar(t, BANK)
                shift_step(t, 0, BANK, y)
                shift_on_gpsimd(t, BANK)
            elif t == TILES - 1:
                shift_step(t, 0, BANK, y)
                shift_step(t, BANK, H, y)
            else:
                shift_step(t, 0, H, y)

        def norm_offset(t):
            offset = stats.tile([P, 1], F32)
            nc.scalar.activation(out=offset[:], in_=negmean_of[t][:], func=ACT.Identity, scale=rstd_of[t][:])
            offset_of[t] = offset

        def norm(t):
            z = offload.tile([P, H], F32)
            nc.scalar.activation(
                out=z[:], in_=u_of[t][:], func=ACT.Identity, scale=rstd_of[t][:], bias=offset_of[t][:]
            )
            z_of[t] = z

        def gain_on_gpsimd(t):
            zg = offload.tile([P, H], F32)
            nc.gpsimd.tensor_tensor(out=zg[:], in0=z_of[t][:], in1=gain_sb[:], op=MULT)
            zg_of[t] = zg

        def last_shift_on_gpsimd(t):
            y_late = offload.tile([P, H], F32)
            nc.gpsimd.tensor_tensor(out=y_late[:], in0=zg_of[t][:], in1=shift_sb[:], op=ADD)
            nc.sync.dma_start(out=out_tiles[t], in_=y_late[:])

        def tile_at(step):
            return step if 0 <= step < TILES else None

        addends_until = 1
        for step in range(first_step, TILES + LATE_LAG + 1):
            for t in range(step + FF_LEAD + 1):
                load_ff(t)
                if t <= step + ATTN_LEAD:
                    load_attn(t)
            now = tile_at(step)
            nxt = tile_at(step + MULTIPLY_LEAD)
            previous = tile_at(step - GAIN_LAG)
            last = tile_at(step - SHIFT_LAG)
            late = tile_at(step - LATE_LAG)
            c = quantise_at.get(step)

            made = list(in_psum)
            in_psum.clear()
            for t in regroup_at.get(step, []):
                regroup(t)
            if previous is not None and previous < TILES - 1:
                one_over_std(previous)
            keep_addends(made[:1])

            if nxt is not None:
                multiply(nxt)
            for t in transpose_at.get(step, []):
                transpose(t)
            if step == first_step:
                spread_bias()
            if step == first_step + 1:
                keep_bias()
                spread("gain", gain_ps)
            if step == -1:
                spread("shift", shift_ps)
                turn_bias()
                nc.scalar.copy(out=gain_sb[:], in_=gain_ps[:])
            for h, lead in enumerate(TENSOR_SUM_LEADS):
                t = tile_at(step + lead)
                if t is not None and addend_on_tensor(t):
                    half_addend_on_tensor(t, h)

            if previous is not None and norm_on_scalar(previous):
                norm_offset(previous)
            if now is not None:
                minus_mean(now, residual_add(now))
            keep_addends(made[1:])
            if last is not None and shift_shared_out(last):
                scale_on_scalar(last, 0)
            if previous is not None and norm_on_scalar(previous):
                norm(previous)

            gain_first = c == 4
            if gain_first and not norm_on_scalar(previous):
                gain_step(previous)
            if step == 1:
                nc.vector.tensor_copy(out=shift_sb[:], in_=shift_ps[:])
            due = range(0)
            if c is not None:
                quantise(c)
                if c == 0:
                    addend_on_vector(0)
                until = last_of[c] + (1 if c in (1, 2) else 2)
                due = range(addends_until, until)
                addends_until = until
            for t in due[:1]:
                addend_on_gpsimd(t)
            if now is not None:
                sum_of_squares(now)
                if now == TILES - 1:
                    one_over_std(now)
            if step == 0:
                keep_turned_bias()
            if last is not None and norm_on_scalar(last):
                gain_on_gpsimd(last)
            if late is not None and norm_on_scalar(late):
                last_shift_on_gpsimd(late)
            if late is not None and shift_shared_out(late):
                shift_on_gpsimd(late, 0)
            for t in due[1:]:
                addend_on_gpsimd(t)
            if previous is not None and not norm_on_scalar(previous) and not gain_first:
                gain_step(previous)
            if last is not None and not norm_on_scalar(last) and not shift_shared_out(last):
                shift_and_store(last)
